import numpy as np
import ml_dtypes


def mxq(x, axis, fmt="e4m3"):
    dtype, down = {"e4m3": (ml_dtypes.float8_e4m3fn, 7), "e5m2": (ml_dtypes.float8_e5m2, 14)}[fmt]
    v = np.moveaxis(np.asarray(x, np.float32).astype(ml_dtypes.bfloat16).astype(np.float64), axis, -1)
    blocks = v.reshape(v.shape[:-1] + (-1, 32))
    amax = np.abs(blocks).max(-1, keepdims=True)
    byte = np.maximum(np.where(amax > 0, np.frexp(amax)[1] - 1 + 127, 0) - down, 1)
    scale = np.exp2(byte - 127.0)
    codes = (blocks / scale).astype(np.float32).astype(dtype).astype(np.float64)
    return np.moveaxis((codes * scale).reshape(v.shape), -1, axis)


WIDE = False


def mx_kscale(k):
    if not WIDE:
        return np.ones(k)
    levels = np.array([10, -10, 5, -5, 0])
    a = np.random.permutation(np.resize(levels, k // 512 * 4)).reshape(k // 512, 4)
    idx = np.arange(k)
    return np.exp2(a[idx // 512, idx % 128 // 32])


BF16 = ml_dtypes.bfloat16


def bf(x):
    return np.asarray(x, np.float32).astype(BF16)


def f64(x):
    return np.asarray(x).astype(np.float64)


E2M1 = np.array([0.0, 0.5, 1.0, 1.5, 2.0, 3.0, 4.0, 6.0, -0.0, -0.5, -1.0, -1.5, -2.0, -3.0, -4.0, -6.0])


def pack_weight(w, fmt):
    k, n = w.shape
    w = f64(bf(w)).reshape(k // 32, 32, n)
    amax = np.abs(w).max(1)
    if fmt == "e4m3":
        byte = np.frexp(amax)[1] - 1 + 127 - 7
    else:
        mant, ex = np.frexp(amax / 6.0)
        byte = np.where(mant > 0.5, ex, ex - 1) + 127
    byte = np.clip(np.where(amax > 0, byte, 1), 1, 254)
    scaled = (w * np.exp2(127.0 - byte)[:, None, :]).reshape(k, n).astype(np.float32)
    by_word = np.ascontiguousarray(scaled.reshape(k // 512, 128, 4, n).transpose(0, 1, 3, 2))
    if fmt == "e4m3":
        words = by_word.astype(ml_dtypes.float8_e4m3fn).view(np.uint8)
    else:
        c = by_word.astype(ml_dtypes.float4_e2m1fn).view(np.uint8) & 0xF
        words = c[..., 0::2] | (c[..., 1::2] << 4)
    return np.ascontiguousarray(words), np.ascontiguousarray(byte.astype(np.uint8).reshape(k // 512, 16, n))


def unpack_weight(words, scales, fmt):
    g, p, n, _ = words.shape
    if fmt == "e4m3":
        vals = np.ascontiguousarray(words).view(ml_dtypes.float8_e4m3fn).astype(np.float64)
    else:
        nib = np.empty((g, p, n, 4), np.uint8)
        nib[..., 0::2] = words & 0xF
        nib[..., 1::2] = words >> 4
        vals = E2M1[nib]
    vals = vals * np.repeat(np.exp2(scales.astype(np.float64) - 127.0), 8, axis=1)[..., None]
    return vals.transpose(0, 1, 3, 2).reshape(g * 512, n)


B, K, DIM, MEM = 512, 4, 512, 512
FMT = "e4m3"


def sigmoid(v):
    return 1.0 / (1.0 + np.exp(-v))


def lin(vq, words, scales, b):
    return (vq @ unpack_weight(words, scales, FMT)) + f64(b)


def setup_inputs():
    s, r, t = mx_kscale(DIM), mx_kscale(MEM), mx_kscale(MEM)
    d = {"inputs": bf(np.random.standard_normal((B, DIM)) * s),
         "child_c": bf(np.random.standard_normal((K, B, MEM))),
         "child_h": bf(np.random.standard_normal((K, B, MEM)) * t),
         "child_h_sum": bf(np.random.standard_normal((B, MEM)) * r)}
    for n in ("ix", "fx", "ux", "ox"):
        w = np.random.standard_normal((MEM, DIM)) * 0.7 / np.sqrt(DIM) / s
        d["W_" + n + "_words"], d["W_" + n + "_scales"] = pack_weight(w.T, FMT)
        d["b_" + n] = bf(np.random.standard_normal(MEM) * 0.5)
    for n in ("ih", "fh", "uh", "oh"):
        w = np.random.standard_normal((MEM, MEM)) * 0.7 / np.sqrt(MEM) / (t if n == "fh" else r)
        d["W_" + n + "_words"], d["W_" + n + "_scales"] = pack_weight(w.T, FMT)
        d["b_" + n] = bf(np.random.standard_normal(MEM) * 0.5)
    return d


def reference(inputs, child_c, child_h, child_h_sum,
              W_ix_words, W_ix_scales, b_ix, W_fx_words, W_fx_scales, b_fx,
              W_ux_words, W_ux_scales, b_ux, W_ox_words, W_ox_scales, b_ox,
              W_ih_words, W_ih_scales, b_ih, W_fh_words, W_fh_scales, b_fh,
              W_uh_words, W_uh_scales, b_uh, W_oh_words, W_oh_scales, b_oh):
    xq = mxq(f64(inputs), 1, "e4m3")
    sq = mxq(f64(child_h_sum), 1, "e4m3")
    hq = mxq(f64(child_h), 2, "e4m3")
    i = sigmoid(lin(xq, W_ix_words, W_ix_scales, b_ix) + lin(sq, W_ih_words, W_ih_scales, b_ih))
    o = sigmoid(lin(xq, W_ox_words, W_ox_scales, b_ox) + lin(sq, W_oh_words, W_oh_scales, b_oh))
    u = np.tanh(lin(xq, W_ux_words, W_ux_scales, b_ux) + lin(sq, W_uh_words, W_uh_scales, b_uh))
    fx = lin(xq, W_fx_words, W_fx_scales, b_fx)
    f = sigmoid(lin(hq, W_fh_words, W_fh_scales, b_fh) + fx[None])
    fc = f * f64(child_c)
    c = i * u + fc.sum(axis=0)
    h = o * np.tanh(c)
    return (c, h)

@@ -1,0 +1,208 @@
+import concourse.mybir as mybir
+from concourse.masks import make_identity
+
+F32 = mybir.dt.float32
+BF16 = mybir.dt.bfloat16
+I32 = mybir.dt.int32
+U32 = mybir.dt.uint32
+U8 = mybir.dt.uint8
+FP8X4 = mybir.dt.float8_e4m3fn_x4
+ACT = mybir.ActivationFunctionType
+ALU = mybir.AluOpType
+
+P = 128
+PACK = 4
+NODES = 512
+WIDTH = 512
+KIDS = 4
+NODE_TILES = NODES // P
+MEM_TILES = WIDTH // P
+
+FLOPS = 2 * NODES * WIDTH * WIDTH * (4 + 3 + KIDS)
+
+
+def load_rows(nc, pool, rows, name):
+    tile = pool.tile([P, NODE_TILES, WIDTH], BF16, name=name)
+    nc.sync.dma_start(out=tile[:], in_=rows.rearrange("(p t) d -> p t d", t=NODE_TILES))
+    return tile
+
+
+def load_weight(nc, pool, planes, slot, words, scales, name):
+    codes = pool.tile([P, WIDTH], U32, name=name + "_codes", align_bytes=64)
+    nc.sync.dma_start(
+        out=codes[:].bitcast(I32),
+        in_=words.rearrange("g p n t -> (g p) (n t)").bitcast(I32),
+    )
+    plane = planes[:, slot, :]
+    rows = scales.rearrange("g (quad r) n -> (g r) quad n", r=4)
+    for r in range(4):
+        nc.sync.dma_start(out=plane[r:P:32, :].bitcast(I32), in_=rows[r].bitcast(I32))
+    return codes, plane
+
+
+def bias_columns(nc, pool, turn_psum, ident, pairs, name):
+    rows = pool.tile([P, 2, P], BF16, name=name + "_rows")
+    nc.vector.memset(rows[:], 0.0)
+    for g, pair in enumerate(pairs):
+        for side, bias in enumerate(pair):
+            nc.gpsimd.dma_start(
+                out=rows[MEM_TILES * g : MEM_TILES * (g + 1), side, :],
+                in_=bias.rearrange("(m c) -> m c", c=P),
+            )
+    summed = pool.tile([P, P], F32, name=name + "_summed")
+    nc.vector.tensor_tensor(out=summed[:], in0=rows[:, 0, :], in1=rows[:, 1, :], op=ALU.add)
+    turned = turn_psum.tile([P, NODE_TILES, P], F32, name="turned", tag="turned")
+    nc.tensor.transpose(turned[:, 0, :], summed[:], ident[:])
+    columns = pool.tile([P, MEM_TILES * len(pairs)], F32, name=name + "_columns")
+    nc.vector.tensor_copy(out=columns[:], in_=turned[:, 0, 0 : MEM_TILES * len(pairs)])
+    return columns
+
+
+def quantise_transposed(nc, keep, stage, turn_psum, ident, rows_sb, name):
+    words = rows_sb[:].bitcast(F32)
+    grouped = stage.tile([P, NODES, PACK], BF16, name="grouped", align_bytes=64)
+    grouped_words = (
+        grouped[:].rearrange("w n t -> w (n t)").bitcast(F32).rearrange("w (n u) -> w n u", u=2)
+    )
+    for half in range(2):
+        turned = turn_psum.tile([P, 2, 2 * P], F32, name="turned", tag="turned")
+        for u in range(2):
+            for j in range(2):
+                nc.tensor.transpose(
+                    turned[:, u, j * P : (j + 1) * P],
+                    words[:, 2 * half + j, u : WIDTH // 2 : 2],
+                    ident[:],
+                )
+        target = grouped_words[:, half * 2 * P : (half + 1) * 2 * P, :]
+        source = turned[:].rearrange("w u n -> w n u")
+        if half == 0:
+            nc.vector.tensor_copy(out=target, in_=source)
+        else:
+            nc.scalar.copy(out=target, in_=source)
+    codes = keep.tile([P, NODES], U32, name=name + "_codes", align_bytes=64)
+    plane = keep.tile([P, NODES], U8, name=name + "_plane", align_bytes=64)
+    nc.vector.quantize_mx(
+        out=codes[:].bitcast(FP8X4),
+        scales=plane[:],
+        in_=grouped[:].rearrange("w n t -> w (n t)"),
+    )
+    return codes, plane
+
+
+def gate(nc, acc_psum, out_sb, func, bias_column, m, products):
+    acc = acc_psum.tile([P, NODES], F32, name="acc")
+    cols = slice(m * P, (m + 1) * P)
+    last = len(products) - 1
+    for step, (weight, moving) in enumerate(products):
+        nc.tensor.matmul_mx(
+            out=acc[:],
+            lhsT=weight[0][:, cols].bitcast(FP8X4),
+            lhsT_scale=weight[1][:, cols],
+            rhs=moving[0][:].bitcast(FP8X4),
+            rhs_scale=moving[1][:],
+            start=(step == 0),
+            stop=(step == last),
+        )
+    nc.scalar.activation(out=out_sb, in_=acc[:], func=func, bias=bias_column, scale=1.0)
+
+
+def turn_back(nc, turn_psum, ident, cells_by_nodes):
+    turned = turn_psum.tile([P, NODE_TILES, P], F32, name="turned", tag="turned")
+    for t in range(NODE_TILES):
+        nc.tensor.transpose(turned[:, t, :], cells_by_nodes[:, t * P : (t + 1) * P], ident[:])
+    return turned
+
+
+def tile_treelstm_pa_kernel(
+    tc, inputs, child_c, child_h, child_h_sum,
+    W_ix_words, W_ix_scales, b_ix, W_fx_words, W_fx_scales, b_fx,
+    W_ux_words, W_ux_scales, b_ux, W_ox_words, W_ox_scales, b_ox,
+    W_ih_words, W_ih_scales, b_ih, W_fh_words, W_fh_scales, b_fh,
+    W_uh_words, W_uh_scales, b_uh, W_oh_words, W_oh_scales, b_oh,
+    out_0, out_1,
+):
+    nc = tc.nc
+    c_out = out_0.rearrange("(p t) m -> p t m", t=NODE_TILES)
+    h_out = out_1.rearrange("(p t) m -> p t m", t=NODE_TILES)
+
+    with tc.tile_pool(name="keep", bufs=1) as keep, tc.tile_pool(
+        name="stage", bufs=2
+    ) as stage, tc.tile_pool(name="work", bufs=3) as work, tc.psum_pool(
+        name="acc_psum", bufs=4
+    ) as acc_psum, tc.psum_pool(name="turn_psum", bufs=4) as turn_psum:
+        ident = keep.tile([P, P], F32, name="ident")
+        make_identity(nc, ident[:])
+
+        planes = keep.tile([P, 8, WIDTH], U8, name="planes", align_bytes=64)
+        nc.vector.memset(planes[:].rearrange("p w n -> p (w n)").bitcast(I32), 0)
+
+        x_sb = load_rows(nc, keep, inputs, "x_sb")
+        w_fx = load_weight(nc, keep, planes, 0, W_fx_words, W_fx_scales, "w_fx")
+        w_fh = load_weight(nc, keep, planes, 1, W_fh_words, W_fh_scales, "w_fh")
+        h_sb = [load_rows(nc, keep, child_h[k], "h_sb%d" % k) for k in range(KIDS)]
+        c_sb = [load_rows(nc, keep, child_c[k], "c_sb%d" % k) for k in range(KIDS)]
+        s_sb = load_rows(nc, keep, child_h_sum, "s_sb")
+        w_ix = load_weight(nc, keep, planes, 2, W_ix_words, W_ix_scales, "w_ix")
+        w_ih = load_weight(nc, keep, planes, 3, W_ih_words, W_ih_scales, "w_ih")
+        w_ux = load_weight(nc, keep, planes, 4, W_ux_words, W_ux_scales, "w_ux")
+        w_uh = load_weight(nc, keep, planes, 5, W_uh_words, W_uh_scales, "w_uh")
+        w_ox = load_weight(nc, keep, planes, 6, W_ox_words, W_ox_scales, "w_ox")
+        w_oh = load_weight(nc, keep, planes, 7, W_oh_words, W_oh_scales, "w_oh")
+
+        x_q = quantise_transposed(nc, keep, stage, turn_psum, ident, x_sb, "x_q")
+        h_q = [
+            quantise_transposed(nc, keep, stage, turn_psum, ident, h_sb[k], "h_q%d" % k)
+            for k in range(KIDS)
+        ]
+
+        f_bias = bias_columns(nc, keep, turn_psum, ident, [(b_fx, b_fh)], "f_bias")
+
+        kids_sum = []
+        for m in range(MEM_TILES):
+            cells = slice(m * P, (m + 1) * P)
+            forget = []
+            for k in range(KIDS):
+                f_t = work.tile([P, NODES], F32, name="f_t%d" % k)
+                gate(nc, acc_psum, f_t[:], ACT.Sigmoid, f_bias[:, m : m + 1], m,
+                     [(w_fx, x_q), (w_fh, h_q[k])])
+                forget.append(f_t)
+            kept = []
+            for k in range(KIDS):
+                f_n = turn_back(nc, turn_psum, ident, forget[k])
+                fc = work.tile([P, NODE_TILES, P], F32, name="fc%d" % k)
+                nc.vector.tensor_tensor(out=fc[:], in0=f_n[:], in1=c_sb[k][:, :, cells], op=ALU.mult)
+                kept.append(fc)
+            nc.vector.tensor_tensor(out=kept[0][:], in0=kept[0][:], in1=kept[1][:], op=ALU.add)
+            nc.vector.tensor_tensor(out=kept[2][:], in0=kept[2][:], in1=kept[3][:], op=ALU.add)
+            total = keep.tile([P, NODE_TILES, P], F32, name="kids_sum%d" % m)
+            nc.vector.tensor_tensor(out=total[:], in0=kept[0][:], in1=kept[2][:], op=ALU.add)
+            kids_sum.append(total)
+
+        iuo_bias = bias_columns(
+            nc, keep, turn_psum, ident, [(b_ix, b_ih), (b_ux, b_uh), (b_ox, b_oh)], "iuo_bias"
+        )
+        s_q = quantise_transposed(nc, keep, stage, turn_psum, ident, s_sb, "s_q")
+
+        for m in range(MEM_TILES):
+            cells = slice(m * P, (m + 1) * P)
+            i_t = work.tile([P, NODES], F32, name="i_t")
+            u_t = work.tile([P, NODES], F32, name="u_t")
+            o_t = work.tile([P, NODES], F32, name="o_t")
+            gate(nc, acc_psum, i_t[:], ACT.Sigmoid, iuo_bias[:, m : m + 1], m,
+                 [(w_ix, x_q), (w_ih, s_q)])
+            gate(nc, acc_psum, u_t[:], ACT.Tanh, iuo_bias[:, MEM_TILES + m : MEM_TILES + m + 1], m,
+                 [(w_ux, x_q), (w_uh, s_q)])
+            gate(nc, acc_psum, o_t[:], ACT.Sigmoid,
+                 iuo_bias[:, 2 * MEM_TILES + m : 2 * MEM_TILES + m + 1], m,
+                 [(w_ox, x_q), (w_oh, s_q)])
+            nc.vector.tensor_tensor(out=i_t[:], in0=i_t[:], in1=u_t[:], op=ALU.mult)
+            iu_n = turn_back(nc, turn_psum, ident, i_t)
+            c_new = work.tile([P, NODE_TILES, P], F32, name="c_new")
+            nc.vector.tensor_tensor(out=c_new[:], in0=iu_n[:], in1=kids_sum[m][:], op=ALU.add)
+            nc.sync.dma_start(out=c_out[:, :, cells], in_=c_new[:])
+            tanh_c = work.tile([P, NODE_TILES, P], F32, name="tanh_c")
+            nc.scalar.activation(out=tanh_c[:], in_=c_new[:], func=ACT.Tanh)
+            o_n = turn_back(nc, turn_psum, ident, o_t)
+            h_new = work.tile([P, NODE_TILES, P], F32, name="h_new")
+            nc.vector.tensor_tensor(out=h_new[:], in0=o_n[:], in1=tanh_c[:], op=ALU.mult)
+            nc.sync.dma_start(out=h_out[:, :, cells], in_=h_new[:])

@@ -27,38 +27,45 @@ def load_rows(nc, pool, rows, name):
     return tile
 
 
-def load_weight(nc, pool, planes, slot, words, scales, name):
-    codes = pool.tile([P, WIDTH], U32, name=name + "_codes", align_bytes=64)
+def load_codes(nc, pool, words, name):
+    codes = pool.tile([P, WIDTH], U32, name=name, align_bytes=64)
     nc.sync.dma_start(
         out=codes[:].bitcast(I32),
         in_=words.rearrange("g p n t -> (g p) (n t)").bitcast(I32),
     )
-    plane = planes[:, slot, :]
+    return codes
+
+
+def load_plane(nc, plane, scales):
     rows = scales.rearrange("g (quad r) n -> (g r) quad n", r=4)
     for r in range(4):
         nc.sync.dma_start(out=plane[r:P:32, :].bitcast(I32), in_=rows[r].bitcast(I32))
-    return codes, plane
+    return plane
 
 
-def bias_columns(nc, pool, turn_psum, ident, pairs, name):
-    rows = pool.tile([P, 2, P], BF16, name=name + "_rows")
+def load_bias_rows(nc, queue, pool, pairs, name):
+    rows = pool.tile([P, 2, P], BF16, name=name)
     nc.vector.memset(rows[:], 0.0)
     for g, pair in enumerate(pairs):
         for side, bias in enumerate(pair):
-            nc.gpsimd.dma_start(
+            queue.dma_start(
                 out=rows[MEM_TILES * g : MEM_TILES * (g + 1), side, :],
                 in_=bias.rearrange("(m c) -> m c", c=P),
             )
+    return rows
+
+
+def bias_columns(nc, pool, turn_psum, ident, rows, count, name):
     summed = pool.tile([P, P], F32, name=name + "_summed")
-    nc.vector.tensor_tensor(out=summed[:], in0=rows[:, 0, :], in1=rows[:, 1, :], op=ALU.add)
+    nc.gpsimd.tensor_tensor(out=summed[:], in0=rows[:, 0, :], in1=rows[:, 1, :], op=ALU.add)
     turned = turn_psum.tile([P, NODE_TILES, P], F32, name="turned", tag="turned")
     nc.tensor.transpose(turned[:, 0, :], summed[:], ident[:])
-    columns = pool.tile([P, MEM_TILES * len(pairs)], F32, name=name + "_columns")
-    nc.vector.tensor_copy(out=columns[:], in_=turned[:, 0, 0 : MEM_TILES * len(pairs)])
+    columns = pool.tile([P, MEM_TILES * count], F32, name=name)
+    nc.scalar.copy(out=columns[:], in_=turned[:, 0, 0 : MEM_TILES * count])
     return columns
 
 
-def quantise_transposed(nc, keep, stage, turn_psum, ident, rows_sb, name):
+def turn_words(nc, stage, turn_psum, ident, rows_sb):
     words = rows_sb[:].bitcast(F32)
     grouped = stage.tile([P, NODES, PACK], BF16, name="grouped", align_bytes=64)
     grouped_words = (
@@ -79,6 +86,10 @@ def quantise_transposed(nc, keep, stage, turn_psum, ident, rows_sb, name):
             nc.vector.tensor_copy(out=target, in_=source)
         else:
             nc.scalar.copy(out=target, in_=source)
+    return grouped
+
+
+def quantise(nc, keep, grouped, name):
     codes = keep.tile([P, NODES], U32, name=name + "_codes", align_bytes=64)
     plane = keep.tile([P, NODES], U8, name=name + "_plane", align_bytes=64)
     nc.vector.quantize_mx(
@@ -126,46 +137,71 @@ def tile_treelstm_pa_kernel(
     h_out = out_1.rearrange("(p t) m -> p t m", t=NODE_TILES)
 
     with tc.tile_pool(name="keep", bufs=1) as keep, tc.tile_pool(
-        name="stage", bufs=2
+        name="stage", bufs=3
     ) as stage, tc.tile_pool(name="work", bufs=3) as work, tc.psum_pool(
         name="acc_psum", bufs=4
-    ) as acc_psum, tc.psum_pool(name="turn_psum", bufs=4) as turn_psum:
+    ) as acc_psum, tc.psum_pool(name="turn_psum", bufs=4) as turn_psum, tc.manual_schedule():
         ident = keep.tile([P, P], F32, name="ident")
         make_identity(nc, ident[:])
-
         planes = keep.tile([P, 8, WIDTH], U8, name="planes", align_bytes=64)
         nc.vector.memset(planes[:].rearrange("p w n -> p (w n)").bitcast(I32), 0)
 
         x_sb = load_rows(nc, keep, inputs, "x_sb")
-        w_fx = load_weight(nc, keep, planes, 0, W_fx_words, W_fx_scales, "w_fx")
-        w_fh = load_weight(nc, keep, planes, 1, W_fh_words, W_fh_scales, "w_fh")
-        h_sb = [load_rows(nc, keep, child_h[k], "h_sb%d" % k) for k in range(KIDS)]
-        c_sb = [load_rows(nc, keep, child_c[k], "c_sb%d" % k) for k in range(KIDS)]
+        f_bias_rows = load_bias_rows(nc, nc.scalar, keep, [(b_fx, b_fh)], "f_bias_rows")
+        fx_codes = load_codes(nc, keep, W_fx_words, "fx_codes")
+        w_fx = (fx_codes, load_plane(nc, planes[:, 0, :], W_fx_scales))
+        fh_codes = load_codes(nc, keep, W_fh_words, "fh_codes")
+        h_sb = [load_rows(nc, keep, child_h[0], "h_sb0")]
+        w_fh = (fh_codes, load_plane(nc, planes[:, 1, :], W_fh_scales))
+        h_sb.append(load_rows(nc, keep, child_h[1], "h_sb1"))
+        h_sb.append(load_rows(nc, keep, child_h[2], "h_sb2"))
+        ix_plane = load_plane(nc, planes[:, 2, :], W_ix_scales)
+        h_sb.append(load_rows(nc, keep, child_h[3], "h_sb3"))
         s_sb = load_rows(nc, keep, child_h_sum, "s_sb")
-        w_ix = load_weight(nc, keep, planes, 2, W_ix_words, W_ix_scales, "w_ix")
-        w_ih = load_weight(nc, keep, planes, 3, W_ih_words, W_ih_scales, "w_ih")
-        w_ux = load_weight(nc, keep, planes, 4, W_ux_words, W_ux_scales, "w_ux")
-        w_uh = load_weight(nc, keep, planes, 5, W_uh_words, W_uh_scales, "w_uh")
-        w_ox = load_weight(nc, keep, planes, 6, W_ox_words, W_ox_scales, "w_ox")
-        w_oh = load_weight(nc, keep, planes, 7, W_oh_words, W_oh_scales, "w_oh")
+        ih_plane = load_plane(nc, planes[:, 3, :], W_ih_scales)
+        c_sb = [load_rows(nc, keep, child_c[0], "c_sb0")]
+        c_sb.append(load_rows(nc, keep, child_c[1], "c_sb1"))
+        ux_plane = load_plane(nc, planes[:, 4, :], W_ux_scales)
+        c_sb.append(load_rows(nc, keep, child_c[2], "c_sb2"))
+        c_sb.append(load_rows(nc, keep, child_c[3], "c_sb3"))
+        uh_plane = load_plane(nc, planes[:, 5, :], W_uh_scales)
+        w_ix = (load_codes(nc, keep, W_ix_words, "ix_codes"), ix_plane)
+        w_ih = (load_codes(nc, keep, W_ih_words, "ih_codes"), ih_plane)
+        ox_plane = load_plane(nc, planes[:, 6, :], W_ox_scales)
+        w_ux = (load_codes(nc, keep, W_ux_words, "ux_codes"), ux_plane)
+        w_uh = (load_codes(nc, keep, W_uh_words, "uh_codes"), uh_plane)
+        oh_plane = load_plane(nc, planes[:, 7, :], W_oh_scales)
+        w_ox = (load_codes(nc, keep, W_ox_words, "ox_codes"), ox_plane)
+        w_oh = (load_codes(nc, keep, W_oh_words, "oh_codes"), oh_plane)
+        iuo_bias_rows = load_bias_rows(
+            nc, nc.gpsimd, keep, [(b_ix, b_ih), (b_ux, b_uh), (b_ox, b_oh)], "iuo_bias_rows"
+        )
 
-        x_q = quantise_transposed(nc, keep, stage, turn_psum, ident, x_sb, "x_q")
-        h_q = [
-            quantise_transposed(nc, keep, stage, turn_psum, ident, h_sb[k], "h_q%d" % k)
-            for k in range(KIDS)
-        ]
+        f_bias = bias_columns(nc, keep, turn_psum, ident, f_bias_rows, 1, "f_bias")
 
-        f_bias = bias_columns(nc, keep, turn_psum, ident, [(b_fx, b_fh)], "f_bias")
+        quantised = []
+        waiting = None
+        for number, rows_sb in enumerate([x_sb] + h_sb + [s_sb]):
+            grouped = turn_words(nc, stage, turn_psum, ident, rows_sb)
+            if waiting is not None:
+                quantised.append(quantise(nc, keep, waiting, "q%d" % (number - 1)))
+            waiting = grouped
+        quantised.append(quantise(nc, keep, waiting, "q%d" % (KIDS + 1)))
+        x_q = quantised[0]
+        h_q = quantised[1 : 1 + KIDS]
+        s_q = quantised[1 + KIDS]
 
-        kids_sum = []
-        for m in range(MEM_TILES):
-            cells = slice(m * P, (m + 1) * P)
+        def forget_gates(m):
             forget = []
             for k in range(KIDS):
                 f_t = work.tile([P, NODES], F32, name="f_t%d" % k)
                 gate(nc, acc_psum, f_t[:], ACT.Sigmoid, f_bias[:, m : m + 1], m,
                      [(w_fx, x_q), (w_fh, h_q[k])])
                 forget.append(f_t)
+            return forget
+
+        def keep_children(m, forget):
+            cells = slice(m * P, (m + 1) * P)
             kept = []
             for k in range(KIDS):
                 f_n = turn_back(nc, turn_psum, ident, forget[k])
@@ -176,15 +212,9 @@ def tile_treelstm_pa_kernel(
             nc.vector.tensor_tensor(out=kept[2][:], in0=kept[2][:], in1=kept[3][:], op=ALU.add)
             total = keep.tile([P, NODE_TILES, P], F32, name="kids_sum%d" % m)
             nc.vector.tensor_tensor(out=total[:], in0=kept[0][:], in1=kept[2][:], op=ALU.add)
-            kids_sum.append(total)
+            return total
 
-        iuo_bias = bias_columns(
-            nc, keep, turn_psum, ident, [(b_ix, b_ih), (b_ux, b_uh), (b_ox, b_oh)], "iuo_bias"
-        )
-        s_q = quantise_transposed(nc, keep, stage, turn_psum, ident, s_sb, "s_q")
-
-        for m in range(MEM_TILES):
-            cells = slice(m * P, (m + 1) * P)
+        def other_gates(m):
             i_t = work.tile([P, NODES], F32, name="i_t")
             u_t = work.tile([P, NODES], F32, name="u_t")
             o_t = work.tile([P, NODES], F32, name="o_t")
@@ -196,13 +226,32 @@ def tile_treelstm_pa_kernel(
                  iuo_bias[:, 2 * MEM_TILES + m : 2 * MEM_TILES + m + 1], m,
                  [(w_ox, x_q), (w_oh, s_q)])
             nc.vector.tensor_tensor(out=i_t[:], in0=i_t[:], in1=u_t[:], op=ALU.mult)
-            iu_n = turn_back(nc, turn_psum, ident, i_t)
+            return i_t, o_t
+
+        def outputs(m, iu_t, o_t, children):
+            cells = slice(m * P, (m + 1) * P)
+            iu_n = turn_back(nc, turn_psum, ident, iu_t)
+            o_n = turn_back(nc, turn_psum, ident, o_t)
             c_new = work.tile([P, NODE_TILES, P], F32, name="c_new")
-            nc.vector.tensor_tensor(out=c_new[:], in0=iu_n[:], in1=kids_sum[m][:], op=ALU.add)
+            nc.vector.tensor_tensor(out=c_new[:], in0=iu_n[:], in1=children[:], op=ALU.add)
             nc.sync.dma_start(out=c_out[:, :, cells], in_=c_new[:])
             tanh_c = work.tile([P, NODE_TILES, P], F32, name="tanh_c")
             nc.scalar.activation(out=tanh_c[:], in_=c_new[:], func=ACT.Tanh)
-            o_n = turn_back(nc, turn_psum, ident, o_t)
             h_new = work.tile([P, NODE_TILES, P], F32, name="h_new")
             nc.vector.tensor_tensor(out=h_new[:], in0=o_n[:], in1=tanh_c[:], op=ALU.mult)
             nc.sync.dma_start(out=h_out[:, :, cells], in_=h_new[:])
+
+        kids_sum = []
+        forget = forget_gates(0)
+        iuo_bias = bias_columns(nc, keep, turn_psum, ident, iuo_bias_rows, 3, "iuo_bias")
+        for m in range(1, MEM_TILES):
+            ahead = forget_gates(m)
+            kids_sum.append(keep_children(m - 1, forget))
+            forget = ahead
+        iu_t, o_t = other_gates(0)
+        kids_sum.append(keep_children(MEM_TILES - 1, forget))
+        for m in range(1, MEM_TILES):
+            ahead = other_gates(m)
+            outputs(m - 1, iu_t, o_t, kids_sum[m - 1])
+            iu_t, o_t = ahead
+        outputs(MEM_TILES - 1, iu_t, o_t, kids_sum[MEM_TILES - 1])

@@ -173,11 +173,11 @@ def tile_treelstm_pa_kernel(
         oh_plane = load_plane(nc, planes[:, 7, :], W_oh_scales)
         w_ox = (load_codes(nc, keep, W_ox_words, "ox_codes"), ox_plane)
         w_oh = (load_codes(nc, keep, W_oh_words, "oh_codes"), oh_plane)
+
+        f_bias = bias_columns(nc, keep, turn_psum, ident, f_bias_rows, 1, "f_bias")
         iuo_bias_rows = load_bias_rows(
             nc, nc.gpsimd, keep, [(b_ix, b_ih), (b_ux, b_uh), (b_ox, b_oh)], "iuo_bias_rows"
         )
-
-        f_bias = bias_columns(nc, keep, turn_psum, ident, f_bias_rows, 1, "f_bias")
 
         quantised = []
         waiting = None
@@ -208,10 +208,10 @@ def tile_treelstm_pa_kernel(
                 fc = work.tile([P, NODE_TILES, P], F32, name="fc%d" % k)
                 nc.vector.tensor_tensor(out=fc[:], in0=f_n[:], in1=c_sb[k][:, :, cells], op=ALU.mult)
                 kept.append(fc)
-            nc.vector.tensor_tensor(out=kept[0][:], in0=kept[0][:], in1=kept[1][:], op=ALU.add)
-            nc.vector.tensor_tensor(out=kept[2][:], in0=kept[2][:], in1=kept[3][:], op=ALU.add)
+            nc.gpsimd.tensor_tensor(out=kept[0][:], in0=kept[0][:], in1=kept[1][:], op=ALU.add)
+            nc.gpsimd.tensor_tensor(out=kept[2][:], in0=kept[2][:], in1=kept[3][:], op=ALU.add)
             total = keep.tile([P, NODE_TILES, P], F32, name="kids_sum%d" % m)
-            nc.vector.tensor_tensor(out=total[:], in0=kept[0][:], in1=kept[2][:], op=ALU.add)
+            nc.gpsimd.tensor_tensor(out=total[:], in0=kept[0][:], in1=kept[2][:], op=ALU.add)
             return total
 
         def other_gates(m):
@@ -225,7 +225,7 @@ def tile_treelstm_pa_kernel(
             gate(nc, acc_psum, o_t[:], ACT.Sigmoid,
                  iuo_bias[:, 2 * MEM_TILES + m : 2 * MEM_TILES + m + 1], m,
                  [(w_ox, x_q), (w_oh, s_q)])
-            nc.vector.tensor_tensor(out=i_t[:], in0=i_t[:], in1=u_t[:], op=ALU.mult)
+            nc.gpsimd.tensor_tensor(out=i_t[:], in0=i_t[:], in1=u_t[:], op=ALU.mult)
             return i_t, o_t
 
         def outputs(m, iu_t, o_t, children):

@@ -36,10 +36,10 @@ def load_codes(nc, pool, words, name):
     return codes
 
 
-def load_plane(nc, plane, scales):
+def load_plane(queue, view, plane, scales):
     rows = scales.rearrange("g (quad r) n -> (g r) quad n", r=4)
     for r in range(4):
-        nc.sync.dma_start(out=plane[r:P:32, :].bitcast(I32), in_=rows[r].bitcast(I32))
+        queue.dma_start(out=plane[r:P:32, :].bitcast(view), in_=rows[r].bitcast(view))
     return plane
 
 
@@ -57,7 +57,7 @@ def load_bias_rows(nc, queue, pool, pairs, name):
 
 def bias_columns(nc, pool, turn_psum, ident, rows, count, name):
     summed = pool.tile([P, P], F32, name=name + "_summed")
-    nc.gpsimd.tensor_tensor(out=summed[:], in0=rows[:, 0, :], in1=rows[:, 1, :], op=ALU.add)
+    nc.vector.tensor_tensor(out=summed[:], in0=rows[:, 0, :], in1=rows[:, 1, :], op=ALU.add)
     turned = turn_psum.tile([P, NODE_TILES, P], F32, name="turned", tag="turned")
     nc.tensor.transpose(turned[:, 0, :], summed[:], ident[:])
     columns = pool.tile([P, MEM_TILES * count], F32, name=name)
@@ -146,38 +146,32 @@ def tile_treelstm_pa_kernel(
         planes = keep.tile([P, 8, WIDTH], U8, name="planes", align_bytes=64)
         nc.vector.memset(planes[:].rearrange("p w n -> p (w n)").bitcast(I32), 0)
 
+        w_fx_plane = load_plane(nc.gpsimd, F32, planes[:, 0, :], W_fx_scales)
+        w_fh_plane = load_plane(nc.gpsimd, F32, planes[:, 1, :], W_fh_scales)
         x_sb = load_rows(nc, keep, inputs, "x_sb")
         f_bias_rows = load_bias_rows(nc, nc.scalar, keep, [(b_fx, b_fh)], "f_bias_rows")
-        fx_codes = load_codes(nc, keep, W_fx_words, "fx_codes")
-        w_fx = (fx_codes, load_plane(nc, planes[:, 0, :], W_fx_scales))
-        fh_codes = load_codes(nc, keep, W_fh_words, "fh_codes")
-        h_sb = [load_rows(nc, keep, child_h[0], "h_sb0")]
-        w_fh = (fh_codes, load_plane(nc, planes[:, 1, :], W_fh_scales))
-        h_sb.append(load_rows(nc, keep, child_h[1], "h_sb1"))
-        h_sb.append(load_rows(nc, keep, child_h[2], "h_sb2"))
-        ix_plane = load_plane(nc, planes[:, 2, :], W_ix_scales)
-        h_sb.append(load_rows(nc, keep, child_h[3], "h_sb3"))
+        w_fx = (load_codes(nc, keep, W_fx_words, "fx_codes"), w_fx_plane)
+        w_fh = (load_codes(nc, keep, W_fh_words, "fh_codes"), w_fh_plane)
+        h_sb = [load_rows(nc, keep, child_h[k], "h_sb%d" % k) for k in range(KIDS)]
         s_sb = load_rows(nc, keep, child_h_sum, "s_sb")
-        ih_plane = load_plane(nc, planes[:, 3, :], W_ih_scales)
-        c_sb = [load_rows(nc, keep, child_c[0], "c_sb0")]
-        c_sb.append(load_rows(nc, keep, child_c[1], "c_sb1"))
-        ux_plane = load_plane(nc, planes[:, 4, :], W_ux_scales)
-        c_sb.append(load_rows(nc, keep, child_c[2], "c_sb2"))
-        c_sb.append(load_rows(nc, keep, child_c[3], "c_sb3"))
-        uh_plane = load_plane(nc, planes[:, 5, :], W_uh_scales)
-        w_ix = (load_codes(nc, keep, W_ix_words, "ix_codes"), ix_plane)
-        w_ih = (load_codes(nc, keep, W_ih_words, "ih_codes"), ih_plane)
-        ox_plane = load_plane(nc, planes[:, 6, :], W_ox_scales)
-        w_ux = (load_codes(nc, keep, W_ux_words, "ux_codes"), ux_plane)
-        w_uh = (load_codes(nc, keep, W_uh_words, "uh_codes"), uh_plane)
-        oh_plane = load_plane(nc, planes[:, 7, :], W_oh_scales)
-        w_ox = (load_codes(nc, keep, W_ox_words, "ox_codes"), ox_plane)
-        w_oh = (load_codes(nc, keep, W_oh_words, "oh_codes"), oh_plane)
-
-        f_bias = bias_columns(nc, keep, turn_psum, ident, f_bias_rows, 1, "f_bias")
+        c_sb = [load_rows(nc, keep, child_c[k], "c_sb%d" % k) for k in range(KIDS)]
+        ix_codes = load_codes(nc, keep, W_ix_words, "ix_codes")
+        ih_codes = load_codes(nc, keep, W_ih_words, "ih_codes")
+        ux_codes = load_codes(nc, keep, W_ux_words, "ux_codes")
+        uh_codes = load_codes(nc, keep, W_uh_words, "uh_codes")
+        ox_codes = load_codes(nc, keep, W_ox_words, "ox_codes")
+        oh_codes = load_codes(nc, keep, W_oh_words, "oh_codes")
+        w_ix = (ix_codes, load_plane(nc.sync, I32, planes[:, 2, :], W_ix_scales))
+        w_ih = (ih_codes, load_plane(nc.sync, I32, planes[:, 3, :], W_ih_scales))
+        w_ux = (ux_codes, load_plane(nc.sync, I32, planes[:, 4, :], W_ux_scales))
+        w_uh = (uh_codes, load_plane(nc.sync, I32, planes[:, 5, :], W_uh_scales))
+        w_ox = (ox_codes, load_plane(nc.sync, I32, planes[:, 6, :], W_ox_scales))
+        w_oh = (oh_codes, load_plane(nc.sync, I32, planes[:, 7, :], W_oh_scales))
         iuo_bias_rows = load_bias_rows(
             nc, nc.gpsimd, keep, [(b_ix, b_ih), (b_ux, b_uh), (b_ox, b_oh)], "iuo_bias_rows"
         )
+
+        f_bias = bias_columns(nc, keep, turn_psum, ident, f_bias_rows, 1, "f_bias")
 
         quantised = []
         waiting = None
@@ -243,11 +237,11 @@ def tile_treelstm_pa_kernel(
 
         kids_sum = []
         forget = forget_gates(0)
-        iuo_bias = bias_columns(nc, keep, turn_psum, ident, iuo_bias_rows, 3, "iuo_bias")
         for m in range(1, MEM_TILES):
             ahead = forget_gates(m)
             kids_sum.append(keep_children(m - 1, forget))
             forget = ahead
+        iuo_bias = bias_columns(nc, keep, turn_psum, ident, iuo_bias_rows, 3, "iuo_bias")
         iu_t, o_t = other_gates(0)
         kids_sum.append(keep_children(MEM_TILES - 1, forget))
         for m in range(1, MEM_TILES):

@@ -36,10 +36,10 @@ def load_codes(nc, pool, words, name):
     return codes
 
 
-def load_plane(queue, view, plane, scales):
+def load_plane(nc, plane, scales):
     rows = scales.rearrange("g (quad r) n -> (g r) quad n", r=4)
     for r in range(4):
-        queue.dma_start(out=plane[r:P:32, :].bitcast(view), in_=rows[r].bitcast(view))
+        nc.sync.dma_start(out=plane[r:P:32, :].bitcast(I32), in_=rows[r].bitcast(I32))
     return plane
 
 
@@ -55,9 +55,13 @@ def load_bias_rows(nc, queue, pool, pairs, name):
     return rows
 
 
-def bias_columns(nc, pool, turn_psum, ident, rows, count, name):
-    summed = pool.tile([P, P], F32, name=name + "_summed")
-    nc.vector.tensor_tensor(out=summed[:], in0=rows[:, 0, :], in1=rows[:, 1, :], op=ALU.add)
+def sum_bias_rows(nc, pool, rows, name):
+    summed = pool.tile([P, P], F32, name=name)
+    nc.gpsimd.tensor_tensor(out=summed[:], in0=rows[:, 0, :], in1=rows[:, 1, :], op=ALU.add)
+    return summed
+
+
+def bias_columns(nc, pool, turn_psum, ident, summed, count, name):
     turned = turn_psum.tile([P, NODE_TILES, P], F32, name="turned", tag="turned")
     nc.tensor.transpose(turned[:, 0, :], summed[:], ident[:])
     columns = pool.tile([P, MEM_TILES * count], F32, name=name)
@@ -146,32 +150,38 @@ def tile_treelstm_pa_kernel(
         planes = keep.tile([P, 8, WIDTH], U8, name="planes", align_bytes=64)
         nc.vector.memset(planes[:].rearrange("p w n -> p (w n)").bitcast(I32), 0)
 
-        w_fx_plane = load_plane(nc.gpsimd, F32, planes[:, 0, :], W_fx_scales)
-        w_fh_plane = load_plane(nc.gpsimd, F32, planes[:, 1, :], W_fh_scales)
         x_sb = load_rows(nc, keep, inputs, "x_sb")
         f_bias_rows = load_bias_rows(nc, nc.scalar, keep, [(b_fx, b_fh)], "f_bias_rows")
-        w_fx = (load_codes(nc, keep, W_fx_words, "fx_codes"), w_fx_plane)
-        w_fh = (load_codes(nc, keep, W_fh_words, "fh_codes"), w_fh_plane)
-        h_sb = [load_rows(nc, keep, child_h[k], "h_sb%d" % k) for k in range(KIDS)]
+        fx_codes = load_codes(nc, keep, W_fx_words, "fx_codes")
+        w_fx = (fx_codes, load_plane(nc, planes[:, 0, :], W_fx_scales))
+        fh_codes = load_codes(nc, keep, W_fh_words, "fh_codes")
+        h_sb = [load_rows(nc, keep, child_h[0], "h_sb0")]
+        w_fh = (fh_codes, load_plane(nc, planes[:, 1, :], W_fh_scales))
+        h_sb.append(load_rows(nc, keep, child_h[1], "h_sb1"))
+        h_sb.append(load_rows(nc, keep, child_h[2], "h_sb2"))
+        ix_plane = load_plane(nc, planes[:, 2, :], W_ix_scales)
+        h_sb.append(load_rows(nc, keep, child_h[3], "h_sb3"))
         s_sb = load_rows(nc, keep, child_h_sum, "s_sb")
-        c_sb = [load_rows(nc, keep, child_c[k], "c_sb%d" % k) for k in range(KIDS)]
-        ix_codes = load_codes(nc, keep, W_ix_words, "ix_codes")
-        ih_codes = load_codes(nc, keep, W_ih_words, "ih_codes")
-        ux_codes = load_codes(nc, keep, W_ux_words, "ux_codes")
-        uh_codes = load_codes(nc, keep, W_uh_words, "uh_codes")
-        ox_codes = load_codes(nc, keep, W_ox_words, "ox_codes")
-        oh_codes = load_codes(nc, keep, W_oh_words, "oh_codes")
-        w_ix = (ix_codes, load_plane(nc.sync, I32, planes[:, 2, :], W_ix_scales))
-        w_ih = (ih_codes, load_plane(nc.sync, I32, planes[:, 3, :], W_ih_scales))
-        w_ux = (ux_codes, load_plane(nc.sync, I32, planes[:, 4, :], W_ux_scales))
-        w_uh = (uh_codes, load_plane(nc.sync, I32, planes[:, 5, :], W_uh_scales))
-        w_ox = (ox_codes, load_plane(nc.sync, I32, planes[:, 6, :], W_ox_scales))
-        w_oh = (oh_codes, load_plane(nc.sync, I32, planes[:, 7, :], W_oh_scales))
+        ih_plane = load_plane(nc, planes[:, 3, :], W_ih_scales)
+        c_sb = [load_rows(nc, keep, child_c[0], "c_sb0")]
+        c_sb.append(load_rows(nc, keep, child_c[1], "c_sb1"))
+        ux_plane = load_plane(nc, planes[:, 4, :], W_ux_scales)
+        c_sb.append(load_rows(nc, keep, child_c[2], "c_sb2"))
+        c_sb.append(load_rows(nc, keep, child_c[3], "c_sb3"))
+        uh_plane = load_plane(nc, planes[:, 5, :], W_uh_scales)
+        w_ix = (load_codes(nc, keep, W_ix_words, "ix_codes"), ix_plane)
+        w_ih = (load_codes(nc, keep, W_ih_words, "ih_codes"), ih_plane)
+        ox_plane = load_plane(nc, planes[:, 6, :], W_ox_scales)
+        w_ux = (load_codes(nc, keep, W_ux_words, "ux_codes"), ux_plane)
+        w_uh = (load_codes(nc, keep, W_uh_words, "uh_codes"), uh_plane)
+        oh_plane = load_plane(nc, planes[:, 7, :], W_oh_scales)
+        w_ox = (load_codes(nc, keep, W_ox_words, "ox_codes"), ox_plane)
+        w_oh = (load_codes(nc, keep, W_oh_words, "oh_codes"), oh_plane)
+        f_bias_sum = sum_bias_rows(nc, keep, f_bias_rows, "f_bias_sum")
         iuo_bias_rows = load_bias_rows(
             nc, nc.gpsimd, keep, [(b_ix, b_ih), (b_ux, b_uh), (b_ox, b_oh)], "iuo_bias_rows"
         )
-
-        f_bias = bias_columns(nc, keep, turn_psum, ident, f_bias_rows, 1, "f_bias")
+        iuo_bias_sum = sum_bias_rows(nc, keep, iuo_bias_rows, "iuo_bias_sum")
 
         quantised = []
         waiting = None
@@ -184,6 +194,7 @@ def tile_treelstm_pa_kernel(
         x_q = quantised[0]
         h_q = quantised[1 : 1 + KIDS]
         s_q = quantised[1 + KIDS]
+        f_bias = bias_columns(nc, keep, turn_psum, ident, f_bias_sum, 1, "f_bias")
 
         def forget_gates(m):
             forget = []
@@ -208,44 +219,52 @@ def tile_treelstm_pa_kernel(
             nc.gpsimd.tensor_tensor(out=total[:], in0=kept[0][:], in1=kept[2][:], op=ALU.add)
             return total
 
-        def other_gates(m):
-            i_t = work.tile([P, NODES], F32, name="i_t")
+        def input_update_gates(m):
+            iu_t = keep.tile([P, NODES], F32, name="iu_t%d" % m)
             u_t = work.tile([P, NODES], F32, name="u_t")
-            o_t = work.tile([P, NODES], F32, name="o_t")
-            gate(nc, acc_psum, i_t[:], ACT.Sigmoid, iuo_bias[:, m : m + 1], m,
+            gate(nc, acc_psum, iu_t[:], ACT.Sigmoid, iuo_bias[:, m : m + 1], m,
                  [(w_ix, x_q), (w_ih, s_q)])
             gate(nc, acc_psum, u_t[:], ACT.Tanh, iuo_bias[:, MEM_TILES + m : MEM_TILES + m + 1], m,
                  [(w_ux, x_q), (w_uh, s_q)])
+            nc.vector.tensor_tensor(out=iu_t[:], in0=iu_t[:], in1=u_t[:], op=ALU.mult)
+            return iu_t
+
+        def cell_state(m):
+            iu_n = turn_back(nc, turn_psum, ident, iu_t[m])
+            c_new = keep.tile([P, NODE_TILES, P], F32, name="c_new%d" % m)
+            nc.vector.tensor_tensor(out=c_new[:], in0=iu_n[:], in1=kids_sum[m][:], op=ALU.add)
+            nc.sync.dma_start(out=c_out[:, :, m * P : (m + 1) * P], in_=c_new[:])
+            tanh_c = keep.tile([P, NODE_TILES, P], F32, name="tanh_c%d" % m)
+            nc.scalar.activation(out=tanh_c[:], in_=c_new[:], func=ACT.Tanh)
+            return tanh_c
+
+        def output_gate(m):
+            o_t = keep.tile([P, NODES], F32, name="o_t%d" % m)
             gate(nc, acc_psum, o_t[:], ACT.Sigmoid,
                  iuo_bias[:, 2 * MEM_TILES + m : 2 * MEM_TILES + m + 1], m,
                  [(w_ox, x_q), (w_oh, s_q)])
-            nc.gpsimd.tensor_tensor(out=i_t[:], in0=i_t[:], in1=u_t[:], op=ALU.mult)
-            return i_t, o_t
+            return o_t
 
-        def outputs(m, iu_t, o_t, children):
-            cells = slice(m * P, (m + 1) * P)
-            iu_n = turn_back(nc, turn_psum, ident, iu_t)
-            o_n = turn_back(nc, turn_psum, ident, o_t)
-            c_new = work.tile([P, NODE_TILES, P], F32, name="c_new")
-            nc.vector.tensor_tensor(out=c_new[:], in0=iu_n[:], in1=children[:], op=ALU.add)
-            nc.sync.dma_start(out=c_out[:, :, cells], in_=c_new[:])
-            tanh_c = work.tile([P, NODE_TILES, P], F32, name="tanh_c")
-            nc.scalar.activation(out=tanh_c[:], in_=c_new[:], func=ACT.Tanh)
-            h_new = work.tile([P, NODE_TILES, P], F32, name="h_new")
-            nc.vector.tensor_tensor(out=h_new[:], in0=o_n[:], in1=tanh_c[:], op=ALU.mult)
-            nc.sync.dma_start(out=h_out[:, :, cells], in_=h_new[:])
+        def hidden_state(m):
+            o_n = turn_back(nc, turn_psum, ident, o_t[m])
+            h_new = keep.tile([P, NODE_TILES, P], F32, name="h_new%d" % m)
+            nc.vector.tensor_tensor(out=h_new[:], in0=o_n[:], in1=tanh_c[m][:], op=ALU.mult)
+            nc.sync.dma_start(out=h_out[:, :, m * P : (m + 1) * P], in_=h_new[:])
 
         kids_sum = []
         forget = forget_gates(0)
+        iuo_bias = bias_columns(nc, keep, turn_psum, ident, iuo_bias_sum, 3, "iuo_bias")
         for m in range(1, MEM_TILES):
             ahead = forget_gates(m)
             kids_sum.append(keep_children(m - 1, forget))
             forget = ahead
-        iuo_bias = bias_columns(nc, keep, turn_psum, ident, iuo_bias_rows, 3, "iuo_bias")
-        iu_t, o_t = other_gates(0)
+        first_half = range(MEM_TILES // 2)
+        second_half = range(MEM_TILES // 2, MEM_TILES)
+        iu_t = [input_update_gates(m) for m in first_half]
         kids_sum.append(keep_children(MEM_TILES - 1, forget))
-        for m in range(1, MEM_TILES):
-            ahead = other_gates(m)
-            outputs(m - 1, iu_t, o_t, kids_sum[m - 1])
-            iu_t, o_t = ahead
-        outputs(MEM_TILES - 1, iu_t, o_t, kids_sum[MEM_TILES - 1])
+        iu_t.extend([input_update_gates(m) for m in second_half])
+        tanh_c = [cell_state(m) for m in first_half]
+        o_t = [output_gate(m) for m in range(MEM_TILES)]
+        tanh_c.extend([cell_state(m) for m in second_half])
+        for m in range(MEM_TILES):
+            hidden_state(m)

@@ -12,19 +12,24 @@ ALU = mybir.AluOpType
 
 P = 128
 PACK = 4
+PAIRS = 2
+QUADRANT = 32
+LIVE_ROWS = 4
 NODES = 512
 WIDTH = 512
 KIDS = 4
 NODE_TILES = NODES // P
-MEM_TILES = WIDTH // P
+CELL_TILES = WIDTH // P
+TILES_PER_BANK = 2
+WEIGHT_NAMES = ("fx", "fh", "ix", "ih", "ux", "uh", "ox", "oh")
 
 FLOPS = 2 * NODES * WIDTH * WIDTH * (4 + 3 + KIDS)
 
 
 def load_rows(nc, pool, rows, name):
-    tile = pool.tile([P, NODE_TILES, WIDTH], BF16, name=name)
-    nc.sync.dma_start(out=tile[:], in_=rows.rearrange("(p t) d -> p t d", t=NODE_TILES))
-    return tile
+    rows_sb = pool.tile([P, NODE_TILES, WIDTH], BF16, name=name)
+    nc.sync.dma_start(out=rows_sb[:], in_=rows.rearrange("(p t) d -> p t d", t=NODE_TILES))
+    return rows_sb
 
 
 def load_codes(nc, pool, words, name):
@@ -37,82 +42,80 @@ def load_codes(nc, pool, words, name):
 
 
 def load_plane(nc, plane, scales):
-    rows = scales.rearrange("g (quad r) n -> (g r) quad n", r=4)
-    for r in range(4):
-        nc.sync.dma_start(out=plane[r:P:32, :].bitcast(I32), in_=rows[r].bitcast(I32))
-    return plane
+    rows = scales.rearrange("g (quad r) n -> (g r) quad n", r=LIVE_ROWS)
+    for r in range(LIVE_ROWS):
+        nc.sync.dma_start(out=plane[r:P:QUADRANT, :].bitcast(I32), in_=rows[r].bitcast(I32))
 
 
-def load_bias_rows(nc, queue, pool, pairs, name):
-    rows = pool.tile([P, 2, P], BF16, name=name)
+def load_bias_sums(nc, queue, pool, pairs, name):
+    rows = pool.tile([P, 2, P], BF16, name=name + "_rows")
     nc.vector.memset(rows[:], 0.0)
     for g, pair in enumerate(pairs):
         for side, bias in enumerate(pair):
             queue.dma_start(
-                out=rows[MEM_TILES * g : MEM_TILES * (g + 1), side, :],
+                out=rows[CELL_TILES * g : CELL_TILES * (g + 1), side, :],
                 in_=bias.rearrange("(m c) -> m c", c=P),
             )
-    return rows
+    sums = pool.tile([P, P], F32, name=name + "_sums")
+    nc.gpsimd.tensor_tensor(out=sums[:], in0=rows[:, 0, :], in1=rows[:, 1, :], op=ALU.add)
+    return sums
 
 
-def sum_bias_rows(nc, pool, rows, name):
-    summed = pool.tile([P, P], F32, name=name)
-    nc.gpsimd.tensor_tensor(out=summed[:], in0=rows[:, 0, :], in1=rows[:, 1, :], op=ALU.add)
-    return summed
-
-
-def bias_columns(nc, pool, turn_psum, ident, summed, count, name):
-    turned = turn_psum.tile([P, NODE_TILES, P], F32, name="turned", tag="turned")
-    nc.tensor.transpose(turned[:, 0, :], summed[:], ident[:])
-    columns = pool.tile([P, MEM_TILES * count], F32, name=name)
-    nc.scalar.copy(out=columns[:], in_=turned[:, 0, 0 : MEM_TILES * count])
+def bias_columns(nc, pool, flip_psum, ident, sums, gates, name):
+    flipped = flip_psum.tile([P, NODE_TILES, P], F32, name="flipped", tag="flipped")
+    nc.tensor.transpose(flipped[:, 0, :], sums[:], ident[:])
+    columns = pool.tile([P, CELL_TILES * gates], F32, name=name)
+    nc.scalar.copy(out=columns[:], in_=flipped[:, 0, 0 : CELL_TILES * gates])
     return columns
 
 
-def turn_words(nc, stage, turn_psum, ident, rows_sb):
+def transpose_words(nc, stage, flip_psum, ident, rows_sb):
     words = rows_sb[:].bitcast(F32)
     grouped = stage.tile([P, NODES, PACK], BF16, name="grouped", align_bytes=64)
-    grouped_words = (
-        grouped[:].rearrange("w n t -> w (n t)").bitcast(F32).rearrange("w (n u) -> w n u", u=2)
+    grouped_pairs = (
+        grouped[:]
+        .rearrange("p n t -> p (n t)")
+        .bitcast(F32)
+        .rearrange("p (n u) -> p n u", u=PAIRS)
     )
-    for half in range(2):
-        turned = turn_psum.tile([P, 2, 2 * P], F32, name="turned", tag="turned")
-        for u in range(2):
-            for j in range(2):
+    columns_per_bank = TILES_PER_BANK * P
+    for bank in range(NODE_TILES // TILES_PER_BANK):
+        flipped = flip_psum.tile([P, PAIRS, columns_per_bank], F32, name="flipped", tag="flipped")
+        for u in range(PAIRS):
+            for j in range(TILES_PER_BANK):
                 nc.tensor.transpose(
-                    turned[:, u, j * P : (j + 1) * P],
-                    words[:, 2 * half + j, u : WIDTH // 2 : 2],
+                    flipped[:, u, j * P : (j + 1) * P],
+                    words[:, TILES_PER_BANK * bank + j, u : WIDTH // 2 : PAIRS],
                     ident[:],
                 )
-        target = grouped_words[:, half * 2 * P : (half + 1) * 2 * P, :]
-        source = turned[:].rearrange("w u n -> w n u")
-        if half == 0:
-            nc.vector.tensor_copy(out=target, in_=source)
-        else:
-            nc.scalar.copy(out=target, in_=source)
+        copy_out = nc.vector.tensor_copy if bank % 2 == 0 else nc.scalar.copy
+        copy_out(
+            out=grouped_pairs[:, bank * columns_per_bank : (bank + 1) * columns_per_bank, :],
+            in_=flipped[:].rearrange("p u n -> p n u"),
+        )
     return grouped
 
 
-def quantise(nc, keep, grouped, name):
-    codes = keep.tile([P, NODES], U32, name=name + "_codes", align_bytes=64)
-    plane = keep.tile([P, NODES], U8, name=name + "_plane", align_bytes=64)
+def quantise(nc, pool, grouped, name):
+    codes = pool.tile([P, NODES], U32, name=name + "_codes", align_bytes=64)
+    plane = pool.tile([P, NODES], U8, name=name + "_plane", align_bytes=64)
     nc.vector.quantize_mx(
         out=codes[:].bitcast(FP8X4),
         scales=plane[:],
-        in_=grouped[:].rearrange("w n t -> w (n t)"),
+        in_=grouped[:].rearrange("p n t -> p (n t)"),
     )
     return codes, plane
 
 
 def gate(nc, acc_psum, out_sb, func, bias_column, m, products):
     acc = acc_psum.tile([P, NODES], F32, name="acc")
-    cols = slice(m * P, (m + 1) * P)
+    cells = slice(m * P, (m + 1) * P)
     last = len(products) - 1
     for step, (weight, moving) in enumerate(products):
         nc.tensor.matmul_mx(
             out=acc[:],
-            lhsT=weight[0][:, cols].bitcast(FP8X4),
-            lhsT_scale=weight[1][:, cols],
+            lhsT=weight[0][:, cells].bitcast(FP8X4),
+            lhsT_scale=weight[1][:, cells],
             rhs=moving[0][:].bitcast(FP8X4),
             rhs_scale=moving[1][:],
             start=(step == 0),
@@ -121,11 +124,11 @@ def gate(nc, acc_psum, out_sb, func, bias_column, m, products):
     nc.scalar.activation(out=out_sb, in_=acc[:], func=func, bias=bias_column, scale=1.0)
 
 
-def turn_back(nc, turn_psum, ident, cells_by_nodes):
-    turned = turn_psum.tile([P, NODE_TILES, P], F32, name="turned", tag="turned")
+def transpose_back(nc, flip_psum, ident, cells_by_nodes):
+    flipped = flip_psum.tile([P, NODE_TILES, P], F32, name="flipped", tag="flipped")
     for t in range(NODE_TILES):
-        nc.tensor.transpose(turned[:, t, :], cells_by_nodes[:, t * P : (t + 1) * P], ident[:])
-    return turned
+        nc.tensor.transpose(flipped[:, t, :], cells_by_nodes[:, t * P : (t + 1) * P], ident[:])
+    return flipped
 
 
 def tile_treelstm_pa_kernel(
@@ -144,49 +147,53 @@ def tile_treelstm_pa_kernel(
         name="stage", bufs=3
     ) as stage, tc.tile_pool(name="work", bufs=3) as work, tc.psum_pool(
         name="acc_psum", bufs=4
-    ) as acc_psum, tc.psum_pool(name="turn_psum", bufs=4) as turn_psum, tc.manual_schedule():
+    ) as acc_psum, tc.psum_pool(name="flip_psum", bufs=4) as flip_psum, tc.manual_schedule():
         ident = keep.tile([P, P], F32, name="ident")
         make_identity(nc, ident[:])
-        planes = keep.tile([P, 8, WIDTH], U8, name="planes", align_bytes=64)
+
+        planes = keep.tile([P, len(WEIGHT_NAMES), WIDTH], U8, name="planes", align_bytes=64)
         nc.vector.memset(planes[:].rearrange("p w n -> p (w n)").bitcast(I32), 0)
+        plane = {name: planes[:, slot, :] for slot, name in enumerate(WEIGHT_NAMES)}
 
         x_sb = load_rows(nc, keep, inputs, "x_sb")
-        f_bias_rows = load_bias_rows(nc, nc.scalar, keep, [(b_fx, b_fh)], "f_bias_rows")
+        f_bias_sums = load_bias_sums(nc, nc.scalar, keep, [(b_fx, b_fh)], "f_bias")
         fx_codes = load_codes(nc, keep, W_fx_words, "fx_codes")
-        w_fx = (fx_codes, load_plane(nc, planes[:, 0, :], W_fx_scales))
+        load_plane(nc, plane["fx"], W_fx_scales)
         fh_codes = load_codes(nc, keep, W_fh_words, "fh_codes")
         h_sb = [load_rows(nc, keep, child_h[0], "h_sb0")]
-        w_fh = (fh_codes, load_plane(nc, planes[:, 1, :], W_fh_scales))
+        load_plane(nc, plane["fh"], W_fh_scales)
         h_sb.append(load_rows(nc, keep, child_h[1], "h_sb1"))
         h_sb.append(load_rows(nc, keep, child_h[2], "h_sb2"))
-        ix_plane = load_plane(nc, planes[:, 2, :], W_ix_scales)
+        load_plane(nc, plane["ix"], W_ix_scales)
         h_sb.append(load_rows(nc, keep, child_h[3], "h_sb3"))
         s_sb = load_rows(nc, keep, child_h_sum, "s_sb")
-        ih_plane = load_plane(nc, planes[:, 3, :], W_ih_scales)
+        load_plane(nc, plane["ih"], W_ih_scales)
         c_sb = [load_rows(nc, keep, child_c[0], "c_sb0")]
         c_sb.append(load_rows(nc, keep, child_c[1], "c_sb1"))
-        ux_plane = load_plane(nc, planes[:, 4, :], W_ux_scales)
+        load_plane(nc, plane["ux"], W_ux_scales)
         c_sb.append(load_rows(nc, keep, child_c[2], "c_sb2"))
         c_sb.append(load_rows(nc, keep, child_c[3], "c_sb3"))
-        uh_plane = load_plane(nc, planes[:, 5, :], W_uh_scales)
-        w_ix = (load_codes(nc, keep, W_ix_words, "ix_codes"), ix_plane)
-        w_ih = (load_codes(nc, keep, W_ih_words, "ih_codes"), ih_plane)
-        ox_plane = load_plane(nc, planes[:, 6, :], W_ox_scales)
-        w_ux = (load_codes(nc, keep, W_ux_words, "ux_codes"), ux_plane)
-        w_uh = (load_codes(nc, keep, W_uh_words, "uh_codes"), uh_plane)
-        oh_plane = load_plane(nc, planes[:, 7, :], W_oh_scales)
-        w_ox = (load_codes(nc, keep, W_ox_words, "ox_codes"), ox_plane)
-        w_oh = (load_codes(nc, keep, W_oh_words, "oh_codes"), oh_plane)
-        f_bias_sum = sum_bias_rows(nc, keep, f_bias_rows, "f_bias_sum")
-        iuo_bias_rows = load_bias_rows(
-            nc, nc.gpsimd, keep, [(b_ix, b_ih), (b_ux, b_uh), (b_ox, b_oh)], "iuo_bias_rows"
+        load_plane(nc, plane["uh"], W_uh_scales)
+        ix_codes = load_codes(nc, keep, W_ix_words, "ix_codes")
+        ih_codes = load_codes(nc, keep, W_ih_words, "ih_codes")
+        load_plane(nc, plane["ox"], W_ox_scales)
+        ux_codes = load_codes(nc, keep, W_ux_words, "ux_codes")
+        uh_codes = load_codes(nc, keep, W_uh_words, "uh_codes")
+        load_plane(nc, plane["oh"], W_oh_scales)
+        ox_codes = load_codes(nc, keep, W_ox_words, "ox_codes")
+        oh_codes = load_codes(nc, keep, W_oh_words, "oh_codes")
+        iuo_bias_sums = load_bias_sums(
+            nc, nc.gpsimd, keep, [(b_ix, b_ih), (b_ux, b_uh), (b_ox, b_oh)], "iuo_bias"
         )
-        iuo_bias_sum = sum_bias_rows(nc, keep, iuo_bias_rows, "iuo_bias_sum")
+        w_fx, w_fh = (fx_codes, plane["fx"]), (fh_codes, plane["fh"])
+        w_ix, w_ih = (ix_codes, plane["ix"]), (ih_codes, plane["ih"])
+        w_ux, w_uh = (ux_codes, plane["ux"]), (uh_codes, plane["uh"])
+        w_ox, w_oh = (ox_codes, plane["ox"]), (oh_codes, plane["oh"])
 
         quantised = []
         waiting = None
         for number, rows_sb in enumerate([x_sb] + h_sb + [s_sb]):
-            grouped = turn_words(nc, stage, turn_psum, ident, rows_sb)
+            grouped = transpose_words(nc, stage, flip_psum, ident, rows_sb)
             if waiting is not None:
                 quantised.append(quantise(nc, keep, waiting, "q%d" % (number - 1)))
             waiting = grouped
@@ -194,7 +201,6 @@ def tile_treelstm_pa_kernel(
         x_q = quantised[0]
         h_q = quantised[1 : 1 + KIDS]
         s_q = quantised[1 + KIDS]
-        f_bias = bias_columns(nc, keep, turn_psum, ident, f_bias_sum, 1, "f_bias")
 
         def forget_gates(m):
             forget = []
@@ -205,11 +211,11 @@ def tile_treelstm_pa_kernel(
                 forget.append(f_t)
             return forget
 
-        def keep_children(m, forget):
+        def children_sum(m, forget):
             cells = slice(m * P, (m + 1) * P)
             kept = []
             for k in range(KIDS):
-                f_n = turn_back(nc, turn_psum, ident, forget[k])
+                f_n = transpose_back(nc, flip_psum, ident, forget[k])
                 fc = work.tile([P, NODE_TILES, P], F32, name="fc%d" % k)
                 nc.vector.tensor_tensor(out=fc[:], in0=f_n[:], in1=c_sb[k][:, :, cells], op=ALU.mult)
                 kept.append(fc)
@@ -219,52 +225,55 @@ def tile_treelstm_pa_kernel(
             nc.gpsimd.tensor_tensor(out=total[:], in0=kept[0][:], in1=kept[2][:], op=ALU.add)
             return total
 
-        def input_update_gates(m):
-            iu_t = keep.tile([P, NODES], F32, name="iu_t%d" % m)
+        def input_times_update(m):
+            product = keep.tile([P, NODES], F32, name="iu_t%d" % m)
             u_t = work.tile([P, NODES], F32, name="u_t")
-            gate(nc, acc_psum, iu_t[:], ACT.Sigmoid, iuo_bias[:, m : m + 1], m,
+            gate(nc, acc_psum, product[:], ACT.Sigmoid, iuo_bias[:, m : m + 1], m,
                  [(w_ix, x_q), (w_ih, s_q)])
-            gate(nc, acc_psum, u_t[:], ACT.Tanh, iuo_bias[:, MEM_TILES + m : MEM_TILES + m + 1], m,
+            gate(nc, acc_psum, u_t[:], ACT.Tanh,
+                 iuo_bias[:, CELL_TILES + m : CELL_TILES + m + 1], m,
                  [(w_ux, x_q), (w_uh, s_q)])
-            nc.vector.tensor_tensor(out=iu_t[:], in0=iu_t[:], in1=u_t[:], op=ALU.mult)
-            return iu_t
+            nc.vector.tensor_tensor(out=product[:], in0=product[:], in1=u_t[:], op=ALU.mult)
+            return product
 
         def cell_state(m):
-            iu_n = turn_back(nc, turn_psum, ident, iu_t[m])
+            iu_n = transpose_back(nc, flip_psum, ident, iu_t[m])
             c_new = keep.tile([P, NODE_TILES, P], F32, name="c_new%d" % m)
             nc.vector.tensor_tensor(out=c_new[:], in0=iu_n[:], in1=kids_sum[m][:], op=ALU.add)
             nc.sync.dma_start(out=c_out[:, :, m * P : (m + 1) * P], in_=c_new[:])
-            tanh_c = keep.tile([P, NODE_TILES, P], F32, name="tanh_c%d" % m)
-            nc.scalar.activation(out=tanh_c[:], in_=c_new[:], func=ACT.Tanh)
-            return tanh_c
+            squashed = keep.tile([P, NODE_TILES, P], F32, name="tanh_c%d" % m)
+            nc.scalar.activation(out=squashed[:], in_=c_new[:], func=ACT.Tanh)
+            return squashed
 
         def output_gate(m):
-            o_t = keep.tile([P, NODES], F32, name="o_t%d" % m)
-            gate(nc, acc_psum, o_t[:], ACT.Sigmoid,
-                 iuo_bias[:, 2 * MEM_TILES + m : 2 * MEM_TILES + m + 1], m,
+            opened = keep.tile([P, NODES], F32, name="o_t%d" % m)
+            gate(nc, acc_psum, opened[:], ACT.Sigmoid,
+                 iuo_bias[:, 2 * CELL_TILES + m : 2 * CELL_TILES + m + 1], m,
                  [(w_ox, x_q), (w_oh, s_q)])
-            return o_t
+            return opened
 
         def hidden_state(m):
-            o_n = turn_back(nc, turn_psum, ident, o_t[m])
+            o_n = transpose_back(nc, flip_psum, ident, o_t[m])
             h_new = keep.tile([P, NODE_TILES, P], F32, name="h_new%d" % m)
             nc.vector.tensor_tensor(out=h_new[:], in0=o_n[:], in1=tanh_c[m][:], op=ALU.mult)
             nc.sync.dma_start(out=h_out[:, :, m * P : (m + 1) * P], in_=h_new[:])
 
+        f_bias = bias_columns(nc, keep, flip_psum, ident, f_bias_sums, 1, "f_bias")
         kids_sum = []
         forget = forget_gates(0)
-        iuo_bias = bias_columns(nc, keep, turn_psum, ident, iuo_bias_sum, 3, "iuo_bias")
-        for m in range(1, MEM_TILES):
+        for m in range(1, CELL_TILES):
             ahead = forget_gates(m)
-            kids_sum.append(keep_children(m - 1, forget))
+            kids_sum.append(children_sum(m - 1, forget))
             forget = ahead
-        first_half = range(MEM_TILES // 2)
-        second_half = range(MEM_TILES // 2, MEM_TILES)
-        iu_t = [input_update_gates(m) for m in first_half]
-        kids_sum.append(keep_children(MEM_TILES - 1, forget))
-        iu_t.extend([input_update_gates(m) for m in second_half])
+
+        iuo_bias = bias_columns(nc, keep, flip_psum, ident, iuo_bias_sums, 3, "iuo_bias")
+        first_half = range(CELL_TILES // 2)
+        second_half = range(CELL_TILES // 2, CELL_TILES)
+        iu_t = [input_times_update(m) for m in first_half]
+        kids_sum.append(children_sum(CELL_TILES - 1, forget))
+        iu_t.extend([input_times_update(m) for m in second_half])
         tanh_c = [cell_state(m) for m in first_half]
-        o_t = [output_gate(m) for m in range(MEM_TILES)]
+        o_t = [output_gate(m) for m in range(CELL_TILES)]
         tanh_c.extend([cell_state(m) for m in second_half])
-        for m in range(MEM_TILES):
+        for m in range(CELL_TILES):
             hidden_state(m)

@@ -157,6 +157,9 @@ def tile_treelstm_pa_kernel(
 
         x_sb = load_rows(nc, keep, inputs, "x_sb")
         f_bias_sums = load_bias_sums(nc, nc.scalar, keep, [(b_fx, b_fh)], "f_bias")
+        table_warmer = keep.tile([P, 2], F32, name="table_warmer")
+        nc.vector.memset(table_warmer[:], 0.0)
+        nc.scalar.activation(out=table_warmer[:, 1:2], in_=table_warmer[:, 0:1], func=ACT.Sigmoid)
         fx_codes = load_codes(nc, keep, W_fx_words, "fx_codes")
         load_plane(nc, plane["fx"], W_fx_scales)
         fh_codes = load_codes(nc, keep, W_fh_words, "fh_codes")
@@ -166,13 +169,13 @@ def tile_treelstm_pa_kernel(
         h_sb.append(load_rows(nc, keep, child_h[2], "h_sb2"))
         load_plane(nc, plane["ix"], W_ix_scales)
         h_sb.append(load_rows(nc, keep, child_h[3], "h_sb3"))
-        s_sb = load_rows(nc, keep, child_h_sum, "s_sb")
-        load_plane(nc, plane["ih"], W_ih_scales)
         c_sb = [load_rows(nc, keep, child_c[0], "c_sb0")]
+        load_plane(nc, plane["ih"], W_ih_scales)
         c_sb.append(load_rows(nc, keep, child_c[1], "c_sb1"))
-        load_plane(nc, plane["ux"], W_ux_scales)
         c_sb.append(load_rows(nc, keep, child_c[2], "c_sb2"))
+        load_plane(nc, plane["ux"], W_ux_scales)
         c_sb.append(load_rows(nc, keep, child_c[3], "c_sb3"))
+        s_sb = load_rows(nc, keep, child_h_sum, "s_sb")
         load_plane(nc, plane["uh"], W_uh_scales)
         ix_codes = load_codes(nc, keep, W_ix_words, "ix_codes")
         ih_codes = load_codes(nc, keep, W_ih_words, "ih_codes")
@@ -192,15 +195,14 @@ def tile_treelstm_pa_kernel(
 
         quantised = []
         waiting = None
-        for number, rows_sb in enumerate([x_sb] + h_sb + [s_sb]):
+        for number, rows_sb in enumerate([x_sb] + h_sb):
             grouped = transpose_words(nc, stage, flip_psum, ident, rows_sb)
             if waiting is not None:
                 quantised.append(quantise(nc, keep, waiting, "q%d" % (number - 1)))
             waiting = grouped
-        quantised.append(quantise(nc, keep, waiting, "q%d" % (KIDS + 1)))
+        quantised.append(quantise(nc, keep, waiting, "q%d" % KIDS))
         x_q = quantised[0]
         h_q = quantised[1 : 1 + KIDS]
-        s_q = quantised[1 + KIDS]
 
         def forget_gates(m):
             forget = []
@@ -263,6 +265,8 @@ def tile_treelstm_pa_kernel(
         forget = forget_gates(0)
         for m in range(1, CELL_TILES):
             ahead = forget_gates(m)
+            if m == 1:
+                s_q = quantise(nc, keep, transpose_words(nc, stage, flip_psum, ident, s_sb), "q_s")
             kids_sum.append(children_sum(m - 1, forget))
             forget = ahead
 

@@ -23,6 +23,8 @@ CELL_TILES = WIDTH // P
 TILES_PER_BANK = 2
 WEIGHT_NAMES = ("fx", "fh", "ix", "ih", "ux", "uh", "ox", "oh")
 
+MX_ALIGN = 256
+
 FLOPS = 2 * NODES * WIDTH * WIDTH * (4 + 3 + KIDS)
 
 
@@ -33,7 +35,7 @@ def load_rows(nc, pool, rows, name):
 
 
 def load_codes(nc, pool, words, name):
-    codes = pool.tile([P, WIDTH], U32, name=name, align_bytes=64)
+    codes = pool.tile([P, WIDTH], U32, name=name, align_bytes=MX_ALIGN)
     nc.sync.dma_start(
         out=codes[:].bitcast(I32),
         in_=words.rearrange("g p n t -> (g p) (n t)").bitcast(I32),
@@ -71,7 +73,7 @@ def bias_columns(nc, pool, flip_psum, ident, sums, gates, name):
 
 def transpose_words(nc, stage, flip_psum, ident, rows_sb):
     words = rows_sb[:].bitcast(F32)
-    grouped = stage.tile([P, NODES, PACK], BF16, name="grouped", align_bytes=64)
+    grouped = stage.tile([P, NODES, PACK], BF16, name="grouped", align_bytes=MX_ALIGN)
     grouped_pairs = (
         grouped[:]
         .rearrange("p n t -> p (n t)")
@@ -97,8 +99,8 @@ def transpose_words(nc, stage, flip_psum, ident, rows_sb):
 
 
 def quantise(nc, pool, grouped, name):
-    codes = pool.tile([P, NODES], U32, name=name + "_codes", align_bytes=64)
-    plane = pool.tile([P, NODES], U8, name=name + "_plane", align_bytes=64)
+    codes = pool.tile([P, NODES], U32, name=name + "_codes", align_bytes=MX_ALIGN)
+    plane = pool.tile([P, NODES], U8, name=name + "_plane", align_bytes=MX_ALIGN)
     nc.vector.quantize_mx(
         out=codes[:].bitcast(FP8X4),
         scales=plane[:],
@@ -151,7 +153,7 @@ def tile_treelstm_pa_kernel(
         ident = keep.tile([P, P], F32, name="ident")
         make_identity(nc, ident[:])
 
-        planes = keep.tile([P, len(WEIGHT_NAMES), WIDTH], U8, name="planes", align_bytes=64)
+        planes = keep.tile([P, len(WEIGHT_NAMES), WIDTH], U8, name="planes", align_bytes=MX_ALIGN)
         nc.vector.memset(planes[:].rearrange("p w n -> p (w n)").bitcast(I32), 0)
         plane = {name: planes[:, slot, :] for slot, name in enumerate(WEIGHT_NAMES)}
 

@@ -158,7 +158,7 @@ def tile_treelstm_pa_kernel(
         plane = {name: planes[:, slot, :] for slot, name in enumerate(WEIGHT_NAMES)}
 
         x_sb = load_rows(nc, keep, inputs, "x_sb")
-        f_bias_sums = load_bias_sums(nc, nc.scalar, keep, [(b_fx, b_fh)], "f_bias")
+        f_bias_sums = load_bias_sums(nc, nc.gpsimd, keep, [(b_fx, b_fh)], "f_bias")
         table_warmer = keep.tile([P, 2], F32, name="table_warmer")
         nc.vector.memset(table_warmer[:], 0.0)
         nc.scalar.activation(out=table_warmer[:, 1:2], in_=table_warmer[:, 0:1], func=ACT.Sigmoid)

@@ -43,21 +43,25 @@ def load_codes(nc, pool, words, name):
     return codes
 
 
-def load_plane(nc, plane, scales):
+def load_plane(queue, word, plane, scales):
     rows = scales.rearrange("g (quad r) n -> (g r) quad n", r=LIVE_ROWS)
     for r in range(LIVE_ROWS):
-        nc.sync.dma_start(out=plane[r:P:QUADRANT, :].bitcast(I32), in_=rows[r].bitcast(I32))
+        queue.dma_start(out=plane[r:P:QUADRANT, :].bitcast(word), in_=rows[r].bitcast(word))
 
 
-def load_bias_sums(nc, queue, pool, pairs, name):
+def load_bias_rows(nc, pool, pairs, name):
     rows = pool.tile([P, 2, P], BF16, name=name + "_rows")
     nc.vector.memset(rows[:], 0.0)
     for g, pair in enumerate(pairs):
         for side, bias in enumerate(pair):
-            queue.dma_start(
+            nc.gpsimd.dma_start(
                 out=rows[CELL_TILES * g : CELL_TILES * (g + 1), side, :],
                 in_=bias.rearrange("(m c) -> m c", c=P),
             )
+    return rows
+
+
+def add_bias_rows(nc, pool, rows, name):
     sums = pool.tile([P, P], F32, name=name + "_sums")
     nc.gpsimd.tensor_tensor(out=sums[:], in0=rows[:, 0, :], in1=rows[:, 1, :], op=ALU.add)
     return sums
@@ -158,38 +162,38 @@ def tile_treelstm_pa_kernel(
         plane = {name: planes[:, slot, :] for slot, name in enumerate(WEIGHT_NAMES)}
 
         x_sb = load_rows(nc, keep, inputs, "x_sb")
-        f_bias_sums = load_bias_sums(nc, nc.gpsimd, keep, [(b_fx, b_fh)], "f_bias")
+        f_bias_rows = load_bias_rows(nc, keep, [(b_fx, b_fh)], "f_bias")
+        load_plane(nc.gpsimd, F32, plane["fx"], W_fx_scales)
+        f_bias_sums = add_bias_rows(nc, keep, f_bias_rows, "f_bias")
         table_warmer = keep.tile([P, 2], F32, name="table_warmer")
         nc.vector.memset(table_warmer[:], 0.0)
         nc.scalar.activation(out=table_warmer[:, 1:2], in_=table_warmer[:, 0:1], func=ACT.Sigmoid)
         fx_codes = load_codes(nc, keep, W_fx_words, "fx_codes")
-        load_plane(nc, plane["fx"], W_fx_scales)
         fh_codes = load_codes(nc, keep, W_fh_words, "fh_codes")
         h_sb = [load_rows(nc, keep, child_h[0], "h_sb0")]
-        load_plane(nc, plane["fh"], W_fh_scales)
+        load_plane(nc.sync, I32, plane["fh"], W_fh_scales)
         h_sb.append(load_rows(nc, keep, child_h[1], "h_sb1"))
         h_sb.append(load_rows(nc, keep, child_h[2], "h_sb2"))
-        load_plane(nc, plane["ix"], W_ix_scales)
+        load_plane(nc.sync, I32, plane["ix"], W_ix_scales)
         h_sb.append(load_rows(nc, keep, child_h[3], "h_sb3"))
         c_sb = [load_rows(nc, keep, child_c[0], "c_sb0")]
-        load_plane(nc, plane["ih"], W_ih_scales)
+        load_plane(nc.sync, I32, plane["ih"], W_ih_scales)
         c_sb.append(load_rows(nc, keep, child_c[1], "c_sb1"))
         c_sb.append(load_rows(nc, keep, child_c[2], "c_sb2"))
-        load_plane(nc, plane["ux"], W_ux_scales)
+        load_plane(nc.sync, I32, plane["ux"], W_ux_scales)
         c_sb.append(load_rows(nc, keep, child_c[3], "c_sb3"))
         s_sb = load_rows(nc, keep, child_h_sum, "s_sb")
-        load_plane(nc, plane["uh"], W_uh_scales)
+        load_plane(nc.sync, I32, plane["uh"], W_uh_scales)
         ix_codes = load_codes(nc, keep, W_ix_words, "ix_codes")
         ih_codes = load_codes(nc, keep, W_ih_words, "ih_codes")
-        load_plane(nc, plane["ox"], W_ox_scales)
+        load_plane(nc.sync, I32, plane["ox"], W_ox_scales)
         ux_codes = load_codes(nc, keep, W_ux_words, "ux_codes")
         uh_codes = load_codes(nc, keep, W_uh_words, "uh_codes")
-        load_plane(nc, plane["oh"], W_oh_scales)
+        load_plane(nc.sync, I32, plane["oh"], W_oh_scales)
         ox_codes = load_codes(nc, keep, W_ox_words, "ox_codes")
         oh_codes = load_codes(nc, keep, W_oh_words, "oh_codes")
-        iuo_bias_sums = load_bias_sums(
-            nc, nc.gpsimd, keep, [(b_ix, b_ih), (b_ux, b_uh), (b_ox, b_oh)], "iuo_bias"
-        )
+        iuo_bias_rows = load_bias_rows(nc, keep, [(b_ix, b_ih), (b_ux, b_uh), (b_ox, b_oh)], "iuo_bias")
+        iuo_bias_sums = add_bias_rows(nc, keep, iuo_bias_rows, "iuo_bias")
         w_fx, w_fh = (fx_codes, plane["fx"]), (fh_codes, plane["fh"])
         w_ix, w_ih = (ix_codes, plane["ix"]), (ih_codes, plane["ih"])
         w_ux, w_uh = (ux_codes, plane["ux"]), (uh_codes, plane["uh"])

@@ -168,15 +168,17 @@ def tile_treelstm_pa_kernel(
         table_warmer = keep.tile([P, 2], F32, name="table_warmer")
         nc.vector.memset(table_warmer[:], 0.0)
         nc.scalar.activation(out=table_warmer[:, 1:2], in_=table_warmer[:, 0:1], func=ACT.Sigmoid)
+        h_sb = []
+        h_sb.append(load_rows(nc, keep, child_h[0], "h_sb0"))
         fx_codes = load_codes(nc, keep, W_fx_words, "fx_codes")
         fh_codes = load_codes(nc, keep, W_fh_words, "fh_codes")
-        h_sb = [load_rows(nc, keep, child_h[0], "h_sb0")]
         load_plane(nc.sync, I32, plane["fh"], W_fh_scales)
         h_sb.append(load_rows(nc, keep, child_h[1], "h_sb1"))
         h_sb.append(load_rows(nc, keep, child_h[2], "h_sb2"))
-        load_plane(nc.sync, I32, plane["ix"], W_ix_scales)
         h_sb.append(load_rows(nc, keep, child_h[3], "h_sb3"))
-        c_sb = [load_rows(nc, keep, child_c[0], "c_sb0")]
+        load_plane(nc.sync, I32, plane["ix"], W_ix_scales)
+        c_sb = []
+        c_sb.append(load_rows(nc, keep, child_c[0], "c_sb0"))
         load_plane(nc.sync, I32, plane["ih"], W_ih_scales)
         c_sb.append(load_rows(nc, keep, child_c[1], "c_sb1"))
         c_sb.append(load_rows(nc, keep, child_c[2], "c_sb2"))
@@ -271,7 +273,7 @@ def tile_treelstm_pa_kernel(
         forget = forget_gates(0)
         for m in range(1, CELL_TILES):
             ahead = forget_gates(m)
-            if m == 1:
+            if m == 2:
                 s_q = quantise(nc, keep, transpose_words(nc, stage, flip_psum, ident, s_sb), "q_s")
             kids_sum.append(children_sum(m - 1, forget))
             forget = ahead
@@ -282,8 +284,11 @@ def tile_treelstm_pa_kernel(
         iu_t = [input_times_update(m) for m in first_half]
         kids_sum.append(children_sum(CELL_TILES - 1, forget))
         iu_t.extend([input_times_update(m) for m in second_half])
+        o_t = [output_gate(m) for m in first_half]
         tanh_c = [cell_state(m) for m in first_half]
-        o_t = [output_gate(m) for m in range(CELL_TILES)]
+        o_t.extend([output_gate(m) for m in second_half])
+        for m in first_half:
+            hidden_state(m)
         tanh_c.extend([cell_state(m) for m in second_half])
-        for m in range(CELL_TILES):
+        for m in second_half:
             hidden_state(m)

@@ -161,21 +161,25 @@ def tile_treelstm_pa_kernel(
         nc.vector.memset(planes[:].rearrange("p w n -> p (w n)").bitcast(I32), 0)
         plane = {name: planes[:, slot, :] for slot, name in enumerate(WEIGHT_NAMES)}
 
-        x_sb = load_rows(nc, keep, inputs, "x_sb")
+        x_sb = keep.tile([P, NODE_TILES, WIDTH], BF16, name="x_sb")
+        x_rows = inputs.rearrange("(p t) d -> p t d", t=NODE_TILES)
+        for half in range(0, NODE_TILES, TILES_PER_BANK):
+            slots = slice(half, half + TILES_PER_BANK)
+            nc.sync.dma_start(out=x_sb[:, slots, :], in_=x_rows[:, slots, :])
         f_bias_rows = load_bias_rows(nc, keep, [(b_fx, b_fh)], "f_bias")
-        load_plane(nc.gpsimd, F32, plane["fx"], W_fx_scales)
         f_bias_sums = add_bias_rows(nc, keep, f_bias_rows, "f_bias")
         table_warmer = keep.tile([P, 2], F32, name="table_warmer")
         nc.vector.memset(table_warmer[:], 0.0)
         nc.scalar.activation(out=table_warmer[:, 1:2], in_=table_warmer[:, 0:1], func=ACT.Sigmoid)
         h_sb = []
         h_sb.append(load_rows(nc, keep, child_h[0], "h_sb0"))
-        fx_codes = load_codes(nc, keep, W_fx_words, "fx_codes")
-        fh_codes = load_codes(nc, keep, W_fh_words, "fh_codes")
-        load_plane(nc.sync, I32, plane["fh"], W_fh_scales)
         h_sb.append(load_rows(nc, keep, child_h[1], "h_sb1"))
         h_sb.append(load_rows(nc, keep, child_h[2], "h_sb2"))
         h_sb.append(load_rows(nc, keep, child_h[3], "h_sb3"))
+        fx_codes = load_codes(nc, keep, W_fx_words, "fx_codes")
+        fh_codes = load_codes(nc, keep, W_fh_words, "fh_codes")
+        load_plane(nc.sync, I32, plane["fx"], W_fx_scales)
+        load_plane(nc.sync, I32, plane["fh"], W_fh_scales)
         load_plane(nc.sync, I32, plane["ix"], W_ix_scales)
         c_sb = []
         c_sb.append(load_rows(nc, keep, child_c[0], "c_sb0"))
@@ -195,7 +199,6 @@ def tile_treelstm_pa_kernel(
         ox_codes = load_codes(nc, keep, W_ox_words, "ox_codes")
         oh_codes = load_codes(nc, keep, W_oh_words, "oh_codes")
         iuo_bias_rows = load_bias_rows(nc, keep, [(b_ix, b_ih), (b_ux, b_uh), (b_ox, b_oh)], "iuo_bias")
-        iuo_bias_sums = add_bias_rows(nc, keep, iuo_bias_rows, "iuo_bias")
         w_fx, w_fh = (fx_codes, plane["fx"]), (fh_codes, plane["fh"])
         w_ix, w_ih = (ix_codes, plane["ix"]), (ih_codes, plane["ih"])
         w_ux, w_uh = (ux_codes, plane["ux"]), (uh_codes, plane["uh"])
@@ -277,6 +280,8 @@ def tile_treelstm_pa_kernel(
                 s_q = quantise(nc, keep, transpose_words(nc, stage, flip_psum, ident, s_sb), "q_s")
             kids_sum.append(children_sum(m - 1, forget))
             forget = ahead
+            if m == 1:
+                iuo_bias_sums = add_bias_rows(nc, keep, iuo_bias_rows, "iuo_bias")
 
         iuo_bias = bias_columns(nc, keep, flip_psum, ident, iuo_bias_sums, 3, "iuo_bias")
         first_half = range(CELL_TILES // 2)

@@ -156,17 +156,18 @@ def tile_treelstm_pa_kernel(
     ) as acc_psum, tc.psum_pool(name="flip_psum", bufs=4) as flip_psum, tc.manual_schedule():
         ident = keep.tile([P, P], F32, name="ident")
         make_identity(nc, ident[:])
-
+        f_bias_rows = load_bias_rows(nc, keep, [(b_fx, b_fh)], "f_bias")
         planes = keep.tile([P, len(WEIGHT_NAMES), WIDTH], U8, name="planes", align_bytes=MX_ALIGN)
         nc.vector.memset(planes[:].rearrange("p w n -> p (w n)").bitcast(I32), 0)
         plane = {name: planes[:, slot, :] for slot, name in enumerate(WEIGHT_NAMES)}
+        load_plane(nc.gpsimd, F32, plane["fx"], W_fx_scales)
+
 
         x_sb = keep.tile([P, NODE_TILES, WIDTH], BF16, name="x_sb")
         x_rows = inputs.rearrange("(p t) d -> p t d", t=NODE_TILES)
         for half in range(0, NODE_TILES, TILES_PER_BANK):
             slots = slice(half, half + TILES_PER_BANK)
             nc.sync.dma_start(out=x_sb[:, slots, :], in_=x_rows[:, slots, :])
-        f_bias_rows = load_bias_rows(nc, keep, [(b_fx, b_fh)], "f_bias")
         f_bias_sums = add_bias_rows(nc, keep, f_bias_rows, "f_bias")
         table_warmer = keep.tile([P, 2], F32, name="table_warmer")
         nc.vector.memset(table_warmer[:], 0.0)
@@ -178,7 +179,6 @@ def tile_treelstm_pa_kernel(
         h_sb.append(load_rows(nc, keep, child_h[3], "h_sb3"))
         fx_codes = load_codes(nc, keep, W_fx_words, "fx_codes")
         fh_codes = load_codes(nc, keep, W_fh_words, "fh_codes")
-        load_plane(nc.sync, I32, plane["fx"], W_fx_scales)
         load_plane(nc.sync, I32, plane["fh"], W_fh_scales)
         load_plane(nc.sync, I32, plane["ix"], W_ix_scales)
         c_sb = []
@@ -291,9 +291,9 @@ def tile_treelstm_pa_kernel(
         iu_t.extend([input_times_update(m) for m in second_half])
         o_t = [output_gate(m) for m in first_half]
         tanh_c = [cell_state(m) for m in first_half]
-        o_t.extend([output_gate(m) for m in second_half])
         for m in first_half:
             hidden_state(m)
+        o_t.extend([output_gate(m) for m in second_half])
         tanh_c.extend([cell_state(m) for m in second_half])
         for m in second_half:
             hidden_state(m)

import concourse.mybir as mybir
from concourse.masks import make_identity

F32 = mybir.dt.float32
BF16 = mybir.dt.bfloat16
I32 = mybir.dt.int32
U32 = mybir.dt.uint32
U8 = mybir.dt.uint8
FP8X4 = mybir.dt.float8_e4m3fn_x4
ACT = mybir.ActivationFunctionType
ALU = mybir.AluOpType

P = 128
PACK = 4
PAIRS = 2
QUADRANT = 32
LIVE_ROWS = 4
NODES = 512
WIDTH = 512
KIDS = 4
NODE_TILES = NODES // P
CELL_TILES = WIDTH // P
TILES_PER_BANK = 2
WEIGHT_NAMES = ("fx", "fh", "ix", "ih", "ux", "uh", "ox", "oh")

MX_ALIGN = 256

FLOPS = 2 * NODES * WIDTH * WIDTH * (4 + 3 + KIDS)


def load_rows(nc, pool, rows, name):
    rows_sb = pool.tile([P, NODE_TILES, WIDTH], BF16, name=name)
    nc.sync.dma_start(out=rows_sb[:], in_=rows.rearrange("(p t) d -> p t d", t=NODE_TILES))
    return rows_sb


def load_codes(nc, pool, words, name):
    codes = pool.tile([P, WIDTH], U32, name=name, align_bytes=MX_ALIGN)
    nc.sync.dma_start(
        out=codes[:].bitcast(I32),
        in_=words.rearrange("g p n t -> (g p) (n t)").bitcast(I32),
    )
    return codes


def load_plane(queue, word, plane, scales):
    rows = scales.rearrange("g (quad r) n -> (g r) quad n", r=LIVE_ROWS)
    for r in range(LIVE_ROWS):
        queue.dma_start(out=plane[r:P:QUADRANT, :].bitcast(word), in_=rows[r].bitcast(word))


def load_bias_rows(nc, pool, pairs, name):
    rows = pool.tile([P, 2, P], BF16, name=name + "_rows")
    nc.vector.memset(rows[:], 0.0)
    for g, pair in enumerate(pairs):
        for side, bias in enumerate(pair):
            nc.gpsimd.dma_start(
                out=rows[CELL_TILES * g : CELL_TILES * (g + 1), side, :],
                in_=bias.rearrange("(m c) -> m c", c=P),
            )
    return rows


def add_bias_rows(nc, pool, rows, name):
    sums = pool.tile([P, P], F32, name=name + "_sums")
    nc.gpsimd.tensor_tensor(out=sums[:], in0=rows[:, 0, :], in1=rows[:, 1, :], op=ALU.add)
    return sums


def bias_columns(nc, pool, flip_psum, ident, sums, gates, name):
    flipped = flip_psum.tile([P, NODE_TILES, P], F32, name="flipped", tag="flipped")
    nc.tensor.transpose(flipped[:, 0, :], sums[:], ident[:])
    columns = pool.tile([P, CELL_TILES * gates], F32, name=name)
    nc.scalar.copy(out=columns[:], in_=flipped[:, 0, 0 : CELL_TILES * gates])
    return columns


def transpose_words(nc, stage, flip_psum, ident, rows_sb):
    words = rows_sb[:].bitcast(F32)
    grouped = stage.tile([P, NODES, PACK], BF16, name="grouped", align_bytes=MX_ALIGN)
    grouped_pairs = (
        grouped[:]
        .rearrange("p n t -> p (n t)")
        .bitcast(F32)
        .rearrange("p (n u) -> p n u", u=PAIRS)
    )
    columns_per_bank = TILES_PER_BANK * P
    for bank in range(NODE_TILES // TILES_PER_BANK):
        flipped = flip_psum.tile([P, PAIRS, columns_per_bank], F32, name="flipped", tag="flipped")
        for u in range(PAIRS):
            for j in range(TILES_PER_BANK):
                nc.tensor.transpose(
                    flipped[:, u, j * P : (j + 1) * P],
                    words[:, TILES_PER_BANK * bank + j, u : WIDTH // 2 : PAIRS],
                    ident[:],
                )
        copy_out = nc.vector.tensor_copy if bank % 2 == 0 else nc.scalar.copy
        copy_out(
            out=grouped_pairs[:, bank * columns_per_bank : (bank + 1) * columns_per_bank, :],
            in_=flipped[:].rearrange("p u n -> p n u"),
        )
    return grouped


def quantise(nc, pool, grouped, name):
    codes = pool.tile([P, NODES], U32, name=name + "_codes", align_bytes=MX_ALIGN)
    plane = pool.tile([P, NODES], U8, name=name + "_plane", align_bytes=MX_ALIGN)
    nc.vector.quantize_mx(
        out=codes[:].bitcast(FP8X4),
        scales=plane[:],
        in_=grouped[:].rearrange("p n t -> p (n t)"),
    )
    return codes, plane


def gate(nc, acc_psum, out_sb, func, bias_column, m, products):
    acc = acc_psum.tile([P, NODES], F32, name="acc")
    cells = slice(m * P, (m + 1) * P)
    last = len(products) - 1
    for step, (weight, moving) in enumerate(products):
        nc.tensor.matmul_mx(
            out=acc[:],
            lhsT=weight[0][:, cells].bitcast(FP8X4),
            lhsT_scale=weight[1][:, cells],
            rhs=moving[0][:].bitcast(FP8X4),
            rhs_scale=moving[1][:],
            start=(step == 0),
            stop=(step == last),
        )
    nc.scalar.activation(out=out_sb, in_=acc[:], func=func, bias=bias_column, scale=1.0)


def transpose_back(nc, flip_psum, ident, cells_by_nodes):
    flipped = flip_psum.tile([P, NODE_TILES, P], F32, name="flipped", tag="flipped")
    for t in range(NODE_TILES):
        nc.tensor.transpose(flipped[:, t, :], cells_by_nodes[:, t * P : (t + 1) * P], ident[:])
    return flipped


def tile_treelstm_pa_kernel(
    tc, inputs, child_c, child_h, child_h_sum,
    W_ix_words, W_ix_scales, b_ix, W_fx_words, W_fx_scales, b_fx,
    W_ux_words, W_ux_scales, b_ux, W_ox_words, W_ox_scales, b_ox,
    W_ih_words, W_ih_scales, b_ih, W_fh_words, W_fh_scales, b_fh,
    W_uh_words, W_uh_scales, b_uh, W_oh_words, W_oh_scales, b_oh,
    out_0, out_1,
):
    nc = tc.nc
    c_out = out_0.rearrange("(p t) m -> p t m", t=NODE_TILES)
    h_out = out_1.rearrange("(p t) m -> p t m", t=NODE_TILES)

    with tc.tile_pool(name="keep", bufs=1) as keep, tc.tile_pool(
        name="stage", bufs=3
    ) as stage, tc.tile_pool(name="work", bufs=3) as work, tc.psum_pool(
        name="acc_psum", bufs=4
    ) as acc_psum, tc.psum_pool(name="flip_psum", bufs=4) as flip_psum, tc.manual_schedule():
        ident = keep.tile([P, P], F32, name="ident")
        make_identity(nc, ident[:])
        f_bias_rows = load_bias_rows(nc, keep, [(b_fx, b_fh)], "f_bias")
        planes = keep.tile([P, len(WEIGHT_NAMES), WIDTH], U8, name="planes", align_bytes=MX_ALIGN)
        nc.vector.memset(planes[:].rearrange("p w n -> p (w n)").bitcast(I32), 0)
        plane = {name: planes[:, slot, :] for slot, name in enumerate(WEIGHT_NAMES)}
        load_plane(nc.gpsimd, F32, plane["fx"], W_fx_scales)


        x_sb = keep.tile([P, NODE_TILES, WIDTH], BF16, name="x_sb")
        x_rows = inputs.rearrange("(p t) d -> p t d", t=NODE_TILES)
        for half in range(0, NODE_TILES, TILES_PER_BANK):
            slots = slice(half, half + TILES_PER_BANK)
            nc.sync.dma_start(out=x_sb[:, slots, :], in_=x_rows[:, slots, :])
        f_bias_sums = add_bias_rows(nc, keep, f_bias_rows, "f_bias")
        table_warmer = keep.tile([P, 2], F32, name="table_warmer")
        nc.vector.memset(table_warmer[:], 0.0)
        nc.scalar.activation(out=table_warmer[:, 1:2], in_=table_warmer[:, 0:1], func=ACT.Sigmoid)
        h_sb = []
        h_sb.append(load_rows(nc, keep, child_h[0], "h_sb0"))
        h_sb.append(load_rows(nc, keep, child_h[1], "h_sb1"))
        h_sb.append(load_rows(nc, keep, child_h[2], "h_sb2"))
        h_sb.append(load_rows(nc, keep, child_h[3], "h_sb3"))
        fx_codes = load_codes(nc, keep, W_fx_words, "fx_codes")
        fh_codes = load_codes(nc, keep, W_fh_words, "fh_codes")
        load_plane(nc.sync, I32, plane["fh"], W_fh_scales)
        load_plane(nc.sync, I32, plane["ix"], W_ix_scales)
        c_sb = []
        c_sb.append(load_rows(nc, keep, child_c[0], "c_sb0"))
        load_plane(nc.sync, I32, plane["ih"], W_ih_scales)
        c_sb.append(load_rows(nc, keep, child_c[1], "c_sb1"))
        c_sb.append(load_rows(nc, keep, child_c[2], "c_sb2"))
        load_plane(nc.sync, I32, plane["ux"], W_ux_scales)
        c_sb.append(load_rows(nc, keep, child_c[3], "c_sb3"))
        s_sb = load_rows(nc, keep, child_h_sum, "s_sb")
        load_plane(nc.sync, I32, plane["uh"], W_uh_scales)
        ix_codes = load_codes(nc, keep, W_ix_words, "ix_codes")
        ih_codes = load_codes(nc, keep, W_ih_words, "ih_codes")
        load_plane(nc.sync, I32, plane["ox"], W_ox_scales)
        ux_codes = load_codes(nc, keep, W_ux_words, "ux_codes")
        uh_codes = load_codes(nc, keep, W_uh_words, "uh_codes")
        load_plane(nc.sync, I32, plane["oh"], W_oh_scales)
        ox_codes = load_codes(nc, keep, W_ox_words, "ox_codes")
        oh_codes = load_codes(nc, keep, W_oh_words, "oh_codes")
        iuo_bias_rows = load_bias_rows(nc, keep, [(b_ix, b_ih), (b_ux, b_uh), (b_ox, b_oh)], "iuo_bias")
        w_fx, w_fh = (fx_codes, plane["fx"]), (fh_codes, plane["fh"])
        w_ix, w_ih = (ix_codes, plane["ix"]), (ih_codes, plane["ih"])
        w_ux, w_uh = (ux_codes, plane["ux"]), (uh_codes, plane["uh"])
        w_ox, w_oh = (ox_codes, plane["ox"]), (oh_codes, plane["oh"])

        quantised = []
        waiting = None
        for number, rows_sb in enumerate([x_sb] + h_sb):
            grouped = transpose_words(nc, stage, flip_psum, ident, rows_sb)
            if waiting is not None:
                quantised.append(quantise(nc, keep, waiting, "q%d" % (number - 1)))
            waiting = grouped
        quantised.append(quantise(nc, keep, waiting, "q%d" % KIDS))
        x_q = quantised[0]
        h_q = quantised[1 : 1 + KIDS]

        def forget_gates(m):
            forget = []
            for k in range(KIDS):
                f_t = work.tile([P, NODES], F32, name="f_t%d" % k)
                gate(nc, acc_psum, f_t[:], ACT.Sigmoid, f_bias[:, m : m + 1], m,
                     [(w_fx, x_q), (w_fh, h_q[k])])
                forget.append(f_t)
            return forget

        def children_sum(m, forget):
            cells = slice(m * P, (m + 1) * P)
            kept = []
            for k in range(KIDS):
                f_n = transpose_back(nc, flip_psum, ident, forget[k])
                fc = work.tile([P, NODE_TILES, P], F32, name="fc%d" % k)
                nc.vector.tensor_tensor(out=fc[:], in0=f_n[:], in1=c_sb[k][:, :, cells], op=ALU.mult)
                kept.append(fc)
            nc.gpsimd.tensor_tensor(out=kept[0][:], in0=kept[0][:], in1=kept[1][:], op=ALU.add)
            nc.gpsimd.tensor_tensor(out=kept[2][:], in0=kept[2][:], in1=kept[3][:], op=ALU.add)
            total = keep.tile([P, NODE_TILES, P], F32, name="kids_sum%d" % m)
            nc.gpsimd.tensor_tensor(out=total[:], in0=kept[0][:], in1=kept[2][:], op=ALU.add)
            return total

        def input_times_update(m):
            product = keep.tile([P, NODES], F32, name="iu_t%d" % m)
            u_t = work.tile([P, NODES], F32, name="u_t")
            gate(nc, acc_psum, product[:], ACT.Sigmoid, iuo_bias[:, m : m + 1], m,
                 [(w_ix, x_q), (w_ih, s_q)])
            gate(nc, acc_psum, u_t[:], ACT.Tanh,
                 iuo_bias[:, CELL_TILES + m : CELL_TILES + m + 1], m,
                 [(w_ux, x_q), (w_uh, s_q)])
            nc.vector.tensor_tensor(out=product[:], in0=product[:], in1=u_t[:], op=ALU.mult)
            return product

        def cell_state(m):
            iu_n = transpose_back(nc, flip_psum, ident, iu_t[m])
            c_new = keep.tile([P, NODE_TILES, P], F32, name="c_new%d" % m)
            nc.vector.tensor_tensor(out=c_new[:], in0=iu_n[:], in1=kids_sum[m][:], op=ALU.add)
            nc.sync.dma_start(out=c_out[:, :, m * P : (m + 1) * P], in_=c_new[:])
            squashed = keep.tile([P, NODE_TILES, P], F32, name="tanh_c%d" % m)
            nc.scalar.activation(out=squashed[:], in_=c_new[:], func=ACT.Tanh)
            return squashed

        def output_gate(m):
            opened = keep.tile([P, NODES], F32, name="o_t%d" % m)
            gate(nc, acc_psum, opened[:], ACT.Sigmoid,
                 iuo_bias[:, 2 * CELL_TILES + m : 2 * CELL_TILES + m + 1], m,
                 [(w_ox, x_q), (w_oh, s_q)])
            return opened

        def hidden_state(m):
            o_n = transpose_back(nc, flip_psum, ident, o_t[m])
            h_new = keep.tile([P, NODE_TILES, P], F32, name="h_new%d" % m)
            nc.vector.tensor_tensor(out=h_new[:], in0=o_n[:], in1=tanh_c[m][:], op=ALU.mult)
            nc.sync.dma_start(out=h_out[:, :, m * P : (m + 1) * P], in_=h_new[:])

        f_bias = bias_columns(nc, keep, flip_psum, ident, f_bias_sums, 1, "f_bias")
        kids_sum = []
        forget = forget_gates(0)
        for m in range(1, CELL_TILES):
            ahead = forget_gates(m)
            if m == 2:
                s_q = quantise(nc, keep, transpose_words(nc, stage, flip_psum, ident, s_sb), "q_s")
            kids_sum.append(children_sum(m - 1, forget))
            forget = ahead
            if m == 1:
                iuo_bias_sums = add_bias_rows(nc, keep, iuo_bias_rows, "iuo_bias")

        iuo_bias = bias_columns(nc, keep, flip_psum, ident, iuo_bias_sums, 3, "iuo_bias")
        first_half = range(CELL_TILES // 2)
        second_half = range(CELL_TILES // 2, CELL_TILES)
        iu_t = [input_times_update(m) for m in first_half]
        kids_sum.append(children_sum(CELL_TILES - 1, forget))
        iu_t.extend([input_times_update(m) for m in second_half])
        o_t = [output_gate(m) for m in first_half]
        tanh_c = [cell_state(m) for m in first_half]
        for m in first_half:
            hidden_state(m)
        o_t.extend([output_gate(m) for m in second_half])
        tanh_c.extend([cell_state(m) for m in second_half])
        for m in second_half:
            hidden_state(m)
